import numpy as np
import ml_dtypes


def mxq(x, axis, fmt="e4m3"):
    dtype, down = {"e4m3": (ml_dtypes.float8_e4m3fn, 7), "e5m2": (ml_dtypes.float8_e5m2, 14)}[fmt]
    v = np.moveaxis(np.asarray(x, np.float32).astype(ml_dtypes.bfloat16).astype(np.float64), axis, -1)
    blocks = v.reshape(v.shape[:-1] + (-1, 32))
    amax = np.abs(blocks).max(-1, keepdims=True)
    byte = np.maximum(np.where(amax > 0, np.frexp(amax)[1] - 1 + 127, 0) - down, 1)
    scale = np.exp2(byte - 127.0)
    codes = (blocks / scale).astype(np.float32).astype(dtype).astype(np.float64)
    return np.moveaxis((codes * scale).reshape(v.shape), -1, axis)


WIDE = False


def mx_kscale(k):
    if not WIDE:
        return np.ones(k)
    levels = np.array([10, -10, 5, -5, 0])
    a = np.random.permutation(np.resize(levels, k // 512 * 4)).reshape(k // 512, 4)
    idx = np.arange(k)
    return np.exp2(a[idx // 512, idx % 128 // 32])


BF16 = ml_dtypes.bfloat16


def bf(x):
    return np.asarray(x, np.float32).astype(BF16)


def f64(x):
    return np.asarray(x).astype(np.float64)


B, DI, DH, H, DP = 4096, 512, 256, 2, 1536
HD = DH // H
EPS = 1e-5


def sigmoid(v):
    return 1.0 / (1.0 + np.exp(-v))


def setup_inputs():
    s = mx_kscale(DI)
    d = {"x": bf(np.random.standard_normal((B, DI)) * 1.5 + np.random.standard_normal((B, 1)) * 0.5),
         "h_prev": bf(np.random.standard_normal((B, DH)) * 0.5),
         "c_prev": bf(np.random.standard_normal((B, DH))),
         "n_prev": bf(0.5 + np.abs(np.random.standard_normal((B, DH)))),
         "m_prev": bf(np.random.standard_normal((B, DH))),
         "ln_w": bf((1.0 + 0.1 * np.random.standard_normal(DI)) * s),
         "ln_b": bf(0.2 * np.random.standard_normal(DI) * s)}
    for g in "zifo":
        d["W" + g] = bf(np.random.standard_normal((DI, DH)) / np.sqrt(DI) / s[:, None])
        d["b_" + g] = bf(0.2 * np.random.standard_normal(DH))
        d["R" + g] = bf(np.random.standard_normal((H, HD, HD)) / np.sqrt(HD))
        d["rb_" + g] = bf(0.2 * np.random.standard_normal(DH))
    return d


def reference(x, h_prev, c_prev, n_prev, m_prev, ln_w, ln_b,
              Wz, b_z, Rz, rb_z, Wi, b_i, Ri, rb_i, Wf, b_f, Rf, rb_f, Wo, b_o, Ro, rb_o):
    x = f64(x)
    mu = x.mean(-1, keepdims=True)
    var = x.var(-1, keepdims=True)
    xn = (x - mu) / np.sqrt(var + EPS) * f64(ln_w) + f64(ln_b)
    xq = mxq(xn, 1, "e4m3")
    hr = f64(h_prev).reshape(B, H, HD).transpose(1, 0, 2)

    def gate(W, b, R, rb):
        rec = (hr @ f64(R)).transpose(1, 0, 2).reshape(B, DH)
        return (xq @ mxq(f64(W), 0, "e4m3")) + f64(b) + (rec + f64(rb))

    z_t = gate(Wz, b_z, Rz, rb_z)
    i_t = gate(Wi, b_i, Ri, rb_i)
    f_t = gate(Wf, b_f, Rf, rb_f)
    o_t = gate(Wo, b_o, Ro, rb_o)
    zt = np.tanh(z_t)
    ot = sigmoid(o_t)
    mt = np.maximum(f_t + f64(m_prev), i_t)
    it = np.exp(i_t - mt)
    ft = np.exp(f_t + f64(m_prev) - mt)
    ct = ft * f64(c_prev) + it * zt
    nt = ft * f64(n_prev) + it
    ht = ot * (ct / (nt + 1e-13))
    return (ht, ct, nt, mt)

@@ -1,0 +1,298 @@
+from contextlib import ExitStack
+
+import concourse.mybir as mybir
+from concourse.masks import make_identity
+
+F32 = mybir.dt.float32
+BF16 = mybir.dt.bfloat16
+U32 = mybir.dt.uint32
+U8 = mybir.dt.uint8
+FP8X4 = mybir.dt.float8_e4m3fn_x4
+ALU = mybir.AluOpType
+ACT = mybir.ActivationFunctionType
+
+P = 128
+PACK = 4
+ROWS = 4096
+D_IN = 512
+D_HID = 256
+HEADS = 2
+D_HEAD = 128
+GATES = 4
+BLOCKS = GATES * HEADS
+LN_EPS = 1e-5
+DIV_EPS = 1e-13
+
+TILES = 4
+CHUNK = TILES * P
+N_CHUNKS = ROWS // CHUNK
+PAIR = 2
+N_PAIRS = TILES // PAIR
+
+FLOPS = 2 * ROWS * D_IN * GATES * D_HID + 2 * ROWS * D_HEAD * GATES * D_HID
+
+
+def tile_slstmblock_pa_t_kernel(
+    tc, x, h_prev, c_prev, n_prev, m_prev, ln_w, ln_b,
+    Wz, b_z, Rz, rb_z, Wi, b_i, Ri, rb_i, Wf, b_f, Rf, rb_f, Wo, b_o, Ro, rb_o,
+    out_0, out_1, out_2, out_3,
+):
+    nc = tc.nc
+    weights = [Wz, Wi, Wf, Wo]
+    recurrents = [Rz, Ri, Rf, Ro]
+    biases = [b_z, b_i, b_f, b_o]
+    rec_biases = [rb_z, rb_i, rb_f, rb_o]
+    GZ, GI, GF, GO = 0, 1, 2, 3
+
+    def chunk_rows(dram, s):
+        return dram[s * CHUNK:(s + 1) * CHUNK, :].rearrange("(p j) w -> p j w", j=TILES)
+
+    with ExitStack() as stack:
+        const = stack.enter_context(tc.tile_pool(name="const", bufs=1))
+        keep = stack.enter_context(tc.tile_pool(name="keep", bufs=1))
+        work = stack.enter_context(tc.tile_pool(name="work", bufs=2))
+        psum_pre = stack.enter_context(tc.psum_pool(name="psum_pre", bufs=1))
+        psum_rot = stack.enter_context(tc.psum_pool(name="psum_rot", bufs=2))
+
+        ident_f32 = const.tile([P, P], F32)
+        make_identity(nc, ident_f32[:])
+        ident_bf16 = const.tile([P, P], BF16)
+        make_identity(nc, ident_bf16[:])
+        neg_half = const.tile([P, TILES], F32)
+        nc.vector.memset(neg_half[:], -0.5)
+        div_eps = const.tile([P, 1], F32)
+        nc.vector.memset(div_eps[:], DIV_EPS)
+
+        vec_rows = const.tile([P, P], BF16)
+        nc.vector.memset(vec_rows[:], 0.0)
+        nc.scalar.dma_start(out=vec_rows[0:4, :], in_=ln_w.rearrange("(t p) -> t p", p=P))
+        nc.scalar.dma_start(out=vec_rows[4:8, :], in_=ln_b.rearrange("(t p) -> t p", p=P))
+        for g in range(GATES):
+            nc.scalar.dma_start(out=vec_rows[8 + HEADS * g:8 + HEADS * (g + 1), :],
+                                in_=biases[g].rearrange("(h f) -> h f", f=D_HEAD))
+            nc.scalar.dma_start(out=vec_rows[16 + HEADS * g:16 + HEADS * (g + 1), :],
+                                in_=rec_biases[g].rearrange("(h f) -> h f", f=D_HEAD))
+
+        x_tiles = {}
+        h_tiles = {}
+        c_tiles = {}
+        n_tiles = {}
+        m_tiles = {}
+
+        def load_x(s):
+            x_sb = work.tile([P, TILES, D_IN], BF16, tag="x_sb", bufs=3)
+            nc.sync.dma_start(out=x_sb[:], in_=chunk_rows(x, s))
+            x_tiles[s] = x_sb
+
+        def load_state(s):
+            h_sb = work.tile([P, TILES, D_HID], BF16, tag="h_sb")
+            nc.sync.dma_start(out=h_sb[:], in_=chunk_rows(h_prev, s))
+            h_tiles[s] = h_sb
+            m_sb = work.tile([P, TILES, D_HID], BF16, tag="m_sb")
+            nc.sync.dma_start(out=m_sb[:], in_=chunk_rows(m_prev, s))
+            m_tiles[s] = m_sb
+            c_sb = work.tile([P, TILES, D_HID], BF16, tag="c_sb")
+            nc.sync.dma_start(out=c_sb[:], in_=chunk_rows(c_prev, s))
+            c_tiles[s] = c_sb
+            n_sb = work.tile([P, TILES, D_HID], BF16, tag="n_sb")
+            nc.sync.dma_start(out=n_sb[:], in_=chunk_rows(n_prev, s))
+            n_tiles[s] = n_sb
+
+        load_x(0)
+
+        w_codes = const.tile([P, GATES * D_HID], U32, align_bytes=64)
+        w_scales = const.tile([P, GATES * D_HID], U8, align_bytes=64)
+        r_sb = const.tile([P, GATES, HEADS, D_HEAD], BF16)
+        for g in range(GATES):
+            w_raw = work.tile([P, PACK, D_HID], BF16, tag="w_raw")
+            nc.sync.dma_start(out=w_raw[:], in_=weights[g].rearrange("(t p) f -> p t f", p=P))
+            w_grouped = work.tile([P, D_HID, PACK], BF16, tag="w_grouped", align_bytes=64)
+            nc.scalar.copy(out=w_grouped[:], in_=w_raw[:].rearrange("p t f -> p f t"))
+            cols = slice(g * D_HID, (g + 1) * D_HID)
+            nc.vector.quantize_mx(
+                out=w_codes[:, cols].bitcast(FP8X4),
+                scales=w_scales[:, cols],
+                in_=w_grouped[:].rearrange("p f t -> p (f t)"),
+            )
+        load_state(0)
+        for g in range(GATES):
+            nc.sync.dma_start(out=r_sb[:, g, :, :], in_=recurrents[g].rearrange("h k f -> k h f"))
+
+        vec_ps = psum_rot.tile([P, P], BF16, tag="turn")
+        nc.tensor.transpose(vec_ps[:], vec_rows[:], ident_bf16[:])
+        vec_cols = const.tile([P, 24], F32)
+        nc.vector.tensor_copy(out=vec_cols[:], in_=vec_ps[:, 0:24])
+        gain = vec_cols[:, 0:4]
+        shift = vec_cols[:, 4:8]
+        gate_bias = const.tile([P, BLOCKS], F32)
+        nc.vector.tensor_add(out=gate_bias[:], in0=vec_cols[:, 8:16], in1=vec_cols[:, 16:24])
+
+        ct_keep = [keep.tile([P, TILES, D_HID], F32, name="ct_keep%d" % s) for s in range(N_CHUNKS)]
+        nt_keep = [keep.tile([P, TILES, D_HID], F32, name="nt_keep%d" % s) for s in range(N_CHUNKS)]
+        th_keep = [keep.tile([P, TILES, D_HID], F32, name="th_keep%d" % s) for s in range(N_CHUNKS)]
+
+        xh_tiles = {}
+        x_mx = {}
+        ht_tiles = {}
+        mt_tiles = {}
+
+        def normalise(s):
+            x_sb = x_tiles.pop(s)
+            stats = work.tile([P, TILES, 6], F32, tag="stats")
+            mean_var = work.tile([P, TILES, 2], F32, tag="mean_var")
+            for j in range(TILES):
+                nc.vector.bn_stats(out=stats[:, j, :], in_=x_sb[:, j, :])
+                nc.vector.bn_aggr(out=mean_var[:, j, :], in_=stats[:, j, :])
+            neg_mean = work.tile([P, TILES], F32, tag="neg_mean")
+            nc.gpsimd.tensor_scalar(out=neg_mean[:], in0=mean_var[:, :, 0], scalar1=-1.0, scalar2=0.0,
+                                    op0=ALU.mult, op1=ALU.add)
+            var_eps = work.tile([P, TILES], F32, tag="var_eps")
+            nc.gpsimd.tensor_scalar(out=var_eps[:], in0=mean_var[:, :, 1], scalar1=LN_EPS, scalar2=1.0,
+                                    op0=ALU.add, op1=ALU.mult)
+            rstd = work.tile([P, TILES], F32, tag="rstd")
+            nc.gpsimd.tensor_tensor(out=rstd[:], in0=var_eps[:], in1=neg_half[:], op=ALU.pow)
+            xh = []
+            for j in range(TILES):
+                xh_j = work.tile([P, D_IN], F32, tag="xh", bufs=6)
+                nc.gpsimd.tensor_scalar(out=xh_j[:], in0=x_sb[:, j, :],
+                                        scalar1=neg_mean[:, j:j + 1], scalar2=rstd[:, j:j + 1],
+                                        op0=ALU.add, op1=ALU.mult)
+                xh.append(xh_j)
+            xh_tiles[s] = xh
+
+        def quantise_xn(s):
+            xh = xh_tiles.pop(s)
+            xn_planes = work.tile([P, PACK, CHUNK], BF16, tag="xn_planes", bufs=1)
+            for t in range(PACK):
+                turned = psum_rot.tile([P, CHUNK], F32, tag="turn")
+                for j in range(TILES):
+                    nc.tensor.transpose(turned[:, j * P:(j + 1) * P], xh[j][:, t * P:(t + 1) * P],
+                                        ident_f32[:])
+                nc.scalar.activation(out=xn_planes[:, t, :], in_=turned[:], func=ACT.Identity,
+                                     bias=shift[:, t:t + 1], scale=gain[:, t:t + 1])
+            xn_grouped = work.tile([P, CHUNK, PACK], BF16, tag="xn_grouped", bufs=1, align_bytes=64)
+            nc.vector.tensor_copy(out=xn_grouped[:], in_=xn_planes[:].rearrange("p t r -> p r t"))
+            x_codes = work.tile([P, CHUNK], U32, tag="x_codes", align_bytes=64)
+            x_scales = work.tile([P, CHUNK], U8, tag="x_scales", align_bytes=64)
+            nc.vector.quantize_mx(out=x_codes[:].bitcast(FP8X4), scales=x_scales[:],
+                                  in_=xn_grouped[:].rearrange("p r t -> p (r t)"))
+            x_mx[s] = (x_codes, x_scales)
+
+        def turn_h(s):
+            h_sb = h_tiles.pop(s)
+            h_ps = psum_rot.tile([P, HEADS, TILES, P], BF16, tag="turn")
+            for h in range(HEADS):
+                for j in range(TILES):
+                    nc.tensor.transpose(h_ps[:, h, j, :], h_sb[:, j, h * D_HEAD:(h + 1) * D_HEAD],
+                                        ident_bf16[:])
+            h_turned = work.tile([P, HEADS, TILES, P], BF16, tag="h_turned")
+            nc.scalar.copy(out=h_turned[:], in_=h_ps[:])
+            ht_tiles[s] = h_turned
+
+        def gate_products(s):
+            x_codes, x_scales = x_mx.pop(s)
+            mx_turned = work.tile([P, BLOCKS, CHUNK], F32, tag="mx_turned")
+            for blk in range(BLOCKS):
+                cols = slice(blk * P, (blk + 1) * P)
+                mx_ps = psum_rot.tile([P, CHUNK], F32, tag="mx_ps")
+                nc.tensor.matmul_mx(out=mx_ps[:],
+                                    lhsT=w_codes[:, cols].bitcast(FP8X4), lhsT_scale=w_scales[:, cols],
+                                    rhs=x_codes[:].bitcast(FP8X4), rhs_scale=x_scales[:],
+                                    start=True, stop=True)
+                nc.scalar.activation(out=mx_turned[:, blk, :], in_=mx_ps[:], func=ACT.Identity,
+                                     bias=gate_bias[:, blk:blk + 1], scale=1.0)
+            mt_tiles[s] = mx_turned
+
+        m_out = {}
+
+        def gating(s, q):
+            mx_turned = mt_tiles[s]
+            h_turned = ht_tiles[s]
+            tiles = slice(q * PAIR, (q + 1) * PAIR)
+            pre = []
+            for g in range(GATES):
+                pre_g = psum_pre.tile([P, PAIR, D_HID], F32, tag="pre%d" % g, name="pre_g")
+                for jj in range(PAIR):
+                    j = q * PAIR + jj
+                    for h in range(HEADS):
+                        out = pre_g[:, jj, h * D_HEAD:(h + 1) * D_HEAD]
+                        nc.tensor.matmul(out=out, lhsT=mx_turned[:, g * HEADS + h, j * P:(j + 1) * P],
+                                         rhs=ident_f32[:], start=True, stop=False, is_transpose=True)
+                        nc.tensor.matmul(out=out, lhsT=h_turned[:, h, j, :], rhs=r_sb[:, g, h, :],
+                                         start=False, stop=True)
+                pre.append(pre_g)
+            shape = [P, PAIR, D_HID]
+            zt = work.tile(shape, F32, tag="zt")
+            nc.scalar.activation(out=zt[:], in_=pre[GZ][:], func=ACT.Tanh)
+            nc.scalar.activation(out=th_keep[s][:, tiles, :], in_=pre[GO][:], func=ACT.Tanh, scale=0.5)
+            fm = work.tile(shape, F32, tag="fm")
+            nc.vector.tensor_tensor(out=fm[:], in0=pre[GF][:], in1=m_tiles[s][:, tiles, :], op=ALU.add)
+            diff = work.tile(shape, F32, tag="diff")
+            nc.vector.tensor_tensor(out=diff[:], in0=pre[GI][:], in1=fm[:], op=ALU.subtract)
+            if q == 0:
+                m_out[s] = work.tile([P, TILES, D_HID], F32, tag="out_stage", name="m_stage")
+            nc.vector.tensor_tensor(out=m_out[s][:, tiles, :], in0=pre[GI][:], in1=fm[:], op=ALU.max)
+            e_i = work.tile(shape, F32, tag="e_i")
+            nc.scalar.activation(out=e_i[:], in_=diff[:], func=ACT.Exp)
+            e_f = work.tile(shape, F32, tag="e_f")
+            nc.scalar.activation(out=e_f[:], in_=diff[:], func=ACT.Exp, scale=-1.0)
+            ct = ct_keep[s][:, tiles, :]
+            nt = nt_keep[s][:, tiles, :]
+            iz = work.tile(shape, F32, tag="iz", bufs=1)
+            nc.vector.scalar_tensor_tensor(out=ct, in0=e_f[:], scalar=1.0, in1=c_tiles[s][:, tiles, :],
+                                           op0=ALU.min, op1=ALU.mult)
+            nc.vector.scalar_tensor_tensor(out=nt, in0=e_f[:], scalar=1.0, in1=n_tiles[s][:, tiles, :],
+                                           op0=ALU.min, op1=ALU.mult)
+            nc.vector.scalar_tensor_tensor(out=iz[:], in0=e_i[:], scalar=1.0, in1=zt[:],
+                                           op0=ALU.min, op1=ALU.mult)
+            nc.vector.scalar_tensor_tensor(out=nt, in0=e_i[:], scalar=1.0, in1=nt,
+                                           op0=ALU.min, op1=ALU.add)
+            nc.vector.tensor_tensor(out=ct, in0=ct, in1=iz[:], op=ALU.add)
+
+        def store_chunk(s):
+            nc.sync.dma_start(out=chunk_rows(out_3, s), in_=m_out.pop(s)[:])
+            nc.sync.dma_start(out=chunk_rows(out_2, s), in_=nt_keep[s][:])
+            nc.sync.dma_start(out=chunk_rows(out_1, s), in_=ct_keep[s][:])
+
+        normalise(0)
+        load_x(1)
+        quantise_xn(0)
+        turn_h(0)
+        gate_products(0)
+        for s in range(N_CHUNKS):
+            nxt = s + 1
+            if nxt < N_CHUNKS:
+                normalise(nxt)
+                load_state(nxt)
+            if nxt + 1 < N_CHUNKS:
+                load_x(nxt + 1)
+            gating(s, 0)
+            if nxt < N_CHUNKS:
+                quantise_xn(nxt)
+                turn_h(nxt)
+            gating(s, 1)
+            store_chunk(s)
+            if nxt < N_CHUNKS:
+                gate_products(nxt)
+
+        for s in range(N_CHUNKS):
+            h_stage = work.tile([P, TILES, D_HID], F32, tag="out_stage")
+            for q in range(N_PAIRS):
+                tiles = slice(q * PAIR, (q + 1) * PAIR)
+                shape = [P, PAIR, D_HID]
+                rs = work.tile(shape, F32, tag="e_i")
+                nc.scalar.activation(out=rs[:], in_=nt_keep[s][:, tiles, :],
+                                     func=ACT.Abs_reciprocal_sqrt, bias=div_eps[:, 0:1], scale=1.0)
+                rs2 = work.tile(shape, F32, tag="e_f")
+                nc.scalar.activation(out=rs2[:], in_=rs[:], func=ACT.Square)
+                rs4 = work.tile(shape, F32, tag="zt")
+                nc.scalar.activation(out=rs4[:], in_=rs2[:], func=ACT.Square)
+                inv = work.tile(shape, F32, tag="fm")
+                nc.vector.scalar_tensor_tensor(out=inv[:], in0=nt_keep[s][:, tiles, :], scalar=DIV_EPS,
+                                               in1=rs4[:], op0=ALU.add, op1=ALU.mult)
+                quot = work.tile(shape, F32, tag="diff")
+                nc.vector.scalar_tensor_tensor(out=quot[:], in0=ct_keep[s][:, tiles, :], scalar=0.5,
+                                               in1=inv[:], op0=ALU.mult, op1=ALU.mult)
+                nc.vector.scalar_tensor_tensor(out=h_stage[:, tiles, :], in0=th_keep[s][:, tiles, :],
+                                               scalar=1.0, in1=quot[:], op0=ALU.add, op1=ALU.mult)
+            nc.sync.dma_start(out=chunk_rows(out_0, s), in_=h_stage[:])

@@ -27,7 +27,8 @@ TILES = 4
 CHUNK = TILES * P
 N_CHUNKS = ROWS // CHUNK
 PAIR = 2
-N_PAIRS = TILES // PAIR
+PAIRS = TILES // PAIR
+N_PAIRS = ROWS // (PAIR * P)
 
 FLOPS = 2 * ROWS * D_IN * GATES * D_HID + 2 * ROWS * D_HEAD * GATES * D_HID
 
@@ -48,21 +49,36 @@ def tile_slstmblock_pa_t_kernel(
         return dram[s * CHUNK:(s + 1) * CHUNK, :].rearrange("(p j) w -> p j w", j=TILES)
 
     with ExitStack() as stack:
+        stack.enter_context(tc.manual_schedule())
         const = stack.enter_context(tc.tile_pool(name="const", bufs=1))
         keep = stack.enter_context(tc.tile_pool(name="keep", bufs=1))
-        work = stack.enter_context(tc.tile_pool(name="work", bufs=2))
+        loads = stack.enter_context(tc.tile_pool(name="loads", bufs=2))
         psum_pre = stack.enter_context(tc.psum_pool(name="psum_pre", bufs=1))
         psum_rot = stack.enter_context(tc.psum_pool(name="psum_rot", bufs=2))
 
-        ident_f32 = const.tile([P, P], F32)
-        make_identity(nc, ident_f32[:])
-        ident_bf16 = const.tile([P, P], BF16)
-        make_identity(nc, ident_bf16[:])
-        neg_half = const.tile([P, TILES], F32)
-        nc.vector.memset(neg_half[:], -0.5)
-        div_eps = const.tile([P, 1], F32)
-        nc.vector.memset(div_eps[:], DIV_EPS)
+        x_tiles = {}
+        h_tiles = {}
+        c_tiles = {}
+        n_tiles = {}
+        m_tiles = {}
 
+        def load_x(c):
+            x_tiles[c] = loads.tile([P, TILES, D_IN], BF16, tag="x_sb", name="x_sb", bufs=3)
+            nc.sync.dma_start(out=x_tiles[c][:], in_=chunk_rows(x, c))
+
+        def load_h(c):
+            h_tiles[c] = loads.tile([P, TILES, D_HID], BF16, tag="h_sb", name="h_sb")
+            nc.sync.dma_start(out=h_tiles[c][:], in_=chunk_rows(h_prev, c))
+
+        def load_state(c):
+            m_tiles[c] = loads.tile([P, TILES, D_HID], BF16, tag="m_sb", name="m_sb")
+            nc.sync.dma_start(out=m_tiles[c][:], in_=chunk_rows(m_prev, c))
+            c_tiles[c] = loads.tile([P, TILES, D_HID], BF16, tag="c_sb", name="c_sb")
+            nc.sync.dma_start(out=c_tiles[c][:], in_=chunk_rows(c_prev, c))
+            n_tiles[c] = loads.tile([P, TILES, D_HID], BF16, tag="n_sb", name="n_sb")
+            nc.sync.dma_start(out=n_tiles[c][:], in_=chunk_rows(n_prev, c))
+
+        load_x(0)
         vec_rows = const.tile([P, P], BF16)
         nc.vector.memset(vec_rows[:], 0.0)
         nc.scalar.dma_start(out=vec_rows[0:4, :], in_=ln_w.rearrange("(t p) -> t p", p=P))
@@ -72,227 +88,286 @@ def tile_slstmblock_pa_t_kernel(
                                 in_=biases[g].rearrange("(h f) -> h f", f=D_HEAD))
             nc.scalar.dma_start(out=vec_rows[16 + HEADS * g:16 + HEADS * (g + 1), :],
                                 in_=rec_biases[g].rearrange("(h f) -> h f", f=D_HEAD))
-
-        x_tiles = {}
-        h_tiles = {}
-        c_tiles = {}
-        n_tiles = {}
-        m_tiles = {}
-
-        def load_x(s):
-            x_sb = work.tile([P, TILES, D_IN], BF16, tag="x_sb", bufs=3)
-            nc.sync.dma_start(out=x_sb[:], in_=chunk_rows(x, s))
-            x_tiles[s] = x_sb
-
-        def load_state(s):
-            h_sb = work.tile([P, TILES, D_HID], BF16, tag="h_sb")
-            nc.sync.dma_start(out=h_sb[:], in_=chunk_rows(h_prev, s))
-            h_tiles[s] = h_sb
-            m_sb = work.tile([P, TILES, D_HID], BF16, tag="m_sb")
-            nc.sync.dma_start(out=m_sb[:], in_=chunk_rows(m_prev, s))
-            m_tiles[s] = m_sb
-            c_sb = work.tile([P, TILES, D_HID], BF16, tag="c_sb")
-            nc.sync.dma_start(out=c_sb[:], in_=chunk_rows(c_prev, s))
-            c_tiles[s] = c_sb
-            n_sb = work.tile([P, TILES, D_HID], BF16, tag="n_sb")
-            nc.sync.dma_start(out=n_sb[:], in_=chunk_rows(n_prev, s))
-            n_tiles[s] = n_sb
-
-        load_x(0)
+        ident_f32 = const.tile([P, P], F32)
+        make_identity(nc, ident_f32[:])
+        ident_bf16 = const.tile([P, P], BF16)
+        make_identity(nc, ident_bf16[:])
+        neg_half = const.tile([P, TILES], F32)
+        nc.vector.memset(neg_half[:], -0.5)
+        div_eps = const.tile([P, 1], F32)
+        nc.vector.memset(div_eps[:], DIV_EPS)
 
         w_codes = const.tile([P, GATES * D_HID], U32, align_bytes=64)
         w_scales = const.tile([P, GATES * D_HID], U8, align_bytes=64)
         r_sb = const.tile([P, GATES, HEADS, D_HEAD], BF16)
-        for g in range(GATES):
-            w_raw = work.tile([P, PACK, D_HID], BF16, tag="w_raw")
-            nc.sync.dma_start(out=w_raw[:], in_=weights[g].rearrange("(t p) f -> p t f", p=P))
-            w_grouped = work.tile([P, D_HID, PACK], BF16, tag="w_grouped", align_bytes=64)
-            nc.scalar.copy(out=w_grouped[:], in_=w_raw[:].rearrange("p t f -> p f t"))
-            cols = slice(g * D_HID, (g + 1) * D_HID)
-            nc.vector.quantize_mx(
-                out=w_codes[:, cols].bitcast(FP8X4),
-                scales=w_scales[:, cols],
-                in_=w_grouped[:].rearrange("p f t -> p (f t)"),
-            )
-        load_state(0)
-        for g in range(GATES):
-            nc.sync.dma_start(out=r_sb[:, g, :, :], in_=recurrents[g].rearrange("h k f -> k h f"))
-
-        vec_ps = psum_rot.tile([P, P], BF16, tag="turn")
-        nc.tensor.transpose(vec_ps[:], vec_rows[:], ident_bf16[:])
         vec_cols = const.tile([P, 24], F32)
-        nc.vector.tensor_copy(out=vec_cols[:], in_=vec_ps[:, 0:24])
         gain = vec_cols[:, 0:4]
         shift = vec_cols[:, 4:8]
         gate_bias = const.tile([P, BLOCKS], F32)
-        nc.vector.tensor_add(out=gate_bias[:], in0=vec_cols[:, 8:16], in1=vec_cols[:, 16:24])
 
-        ct_keep = [keep.tile([P, TILES, D_HID], F32, name="ct_keep%d" % s) for s in range(N_CHUNKS)]
-        nt_keep = [keep.tile([P, TILES, D_HID], F32, name="nt_keep%d" % s) for s in range(N_CHUNKS)]
-        th_keep = [keep.tile([P, TILES, D_HID], F32, name="th_keep%d" % s) for s in range(N_CHUNKS)]
+        ct_keep = [keep.tile([P, TILES, D_HID], F32, name="ct_keep%d" % c) for c in range(N_CHUNKS)]
+        nt_keep = [keep.tile([P, TILES, D_HID], F32, name="nt_keep%d" % c) for c in range(N_CHUNKS)]
+        th_keep = [keep.tile([P, TILES, D_HID], F32, name="th_keep%d" % c) for c in range(N_CHUNKS)]
 
-        xh_tiles = {}
-        x_mx = {}
-        ht_tiles = {}
-        mt_tiles = {}
+        with ExitStack() as main_stack:
+            work = main_stack.enter_context(tc.tile_pool(name="work", bufs=2))
+            xh_tiles = {}
+            planes = {}
+            x_mx = {}
+            h_turned = {}
+            mx_turned = {}
+            pre = {}
+            gate_tiles = {}
+            m_stage = {}
 
-        def normalise(s):
-            x_sb = x_tiles.pop(s)
-            stats = work.tile([P, TILES, 6], F32, tag="stats")
-            mean_var = work.tile([P, TILES, 2], F32, tag="mean_var")
-            for j in range(TILES):
-                nc.vector.bn_stats(out=stats[:, j, :], in_=x_sb[:, j, :])
-                nc.vector.bn_aggr(out=mean_var[:, j, :], in_=stats[:, j, :])
-            neg_mean = work.tile([P, TILES], F32, tag="neg_mean")
-            nc.gpsimd.tensor_scalar(out=neg_mean[:], in0=mean_var[:, :, 0], scalar1=-1.0, scalar2=0.0,
-                                    op0=ALU.mult, op1=ALU.add)
-            var_eps = work.tile([P, TILES], F32, tag="var_eps")
-            nc.gpsimd.tensor_scalar(out=var_eps[:], in0=mean_var[:, :, 1], scalar1=LN_EPS, scalar2=1.0,
-                                    op0=ALU.add, op1=ALU.mult)
-            rstd = work.tile([P, TILES], F32, tag="rstd")
-            nc.gpsimd.tensor_tensor(out=rstd[:], in0=var_eps[:], in1=neg_half[:], op=ALU.pow)
-            xh = []
-            for j in range(TILES):
-                xh_j = work.tile([P, D_IN], F32, tag="xh", bufs=6)
-                nc.gpsimd.tensor_scalar(out=xh_j[:], in0=x_sb[:, j, :],
-                                        scalar1=neg_mean[:, j:j + 1], scalar2=rstd[:, j:j + 1],
-                                        op0=ALU.add, op1=ALU.mult)
-                xh.append(xh_j)
-            xh_tiles[s] = xh
+            def normalise(c):
+                x_sb = x_tiles.pop(c)
+                stats = work.tile([P, TILES, 6], F32, tag="stats")
+                mean_var = work.tile([P, TILES, 2], F32, tag="mean_var")
+                for j in range(TILES):
+                    nc.vector.bn_stats(out=stats[:, j, :], in_=x_sb[:, j, :])
+                for j in range(TILES):
+                    nc.vector.bn_aggr(out=mean_var[:, j, :], in_=stats[:, j, :])
+                var_eps = work.tile([P, TILES], F32, tag="var_eps")
+                nc.vector.tensor_scalar_add(out=var_eps[:], in0=mean_var[:, :, 1], scalar1=LN_EPS)
+                neg_mean = work.tile([P, TILES], F32, tag="neg_mean")
+                nc.vector.tensor_scalar_mul(out=neg_mean[:], in0=mean_var[:, :, 0], scalar1=-1.0)
+                rstd = work.tile([P, TILES], F32, tag="rstd")
+                nc.gpsimd.tensor_tensor(out=rstd[:], in0=var_eps[:], in1=neg_half[:], op=ALU.pow)
+                xh_tiles[c] = []
+                for j in range(TILES):
+                    xh_j = work.tile([P, D_IN], F32, tag="xh", bufs=2 * TILES)
+                    nc.gpsimd.tensor_scalar(out=xh_j[:], in0=x_sb[:, j, :],
+                                            scalar1=neg_mean[:, j:j + 1], scalar2=rstd[:, j:j + 1],
+                                            op0=ALU.add, op1=ALU.mult)
+                    xh_tiles[c].append(xh_j)
 
-        def quantise_xn(s):
-            xh = xh_tiles.pop(s)
-            xn_planes = work.tile([P, PACK, CHUNK], BF16, tag="xn_planes", bufs=1)
-            for t in range(PACK):
+            def turn_xn(c, t):
                 turned = psum_rot.tile([P, CHUNK], F32, tag="turn")
                 for j in range(TILES):
-                    nc.tensor.transpose(turned[:, j * P:(j + 1) * P], xh[j][:, t * P:(t + 1) * P],
-                                        ident_f32[:])
-                nc.scalar.activation(out=xn_planes[:, t, :], in_=turned[:], func=ACT.Identity,
+                    nc.tensor.transpose(turned[:, j * P:(j + 1) * P],
+                                        xh_tiles[c][j][:, t * P:(t + 1) * P], ident_f32[:])
+                return turned
+
+            def scale_xn(c, t, turned):
+                if t == 0:
+                    planes[c] = work.tile([P, PACK, CHUNK], BF16, tag="xn_planes", name="xn_planes")
+                nc.scalar.activation(out=planes[c][:, t, :], in_=turned[:], func=ACT.Identity,
                                      bias=shift[:, t:t + 1], scale=gain[:, t:t + 1])
-            xn_grouped = work.tile([P, CHUNK, PACK], BF16, tag="xn_grouped", bufs=1, align_bytes=64)
-            nc.vector.tensor_copy(out=xn_grouped[:], in_=xn_planes[:].rearrange("p t r -> p r t"))
-            x_codes = work.tile([P, CHUNK], U32, tag="x_codes", align_bytes=64)
-            x_scales = work.tile([P, CHUNK], U8, tag="x_scales", align_bytes=64)
-            nc.vector.quantize_mx(out=x_codes[:].bitcast(FP8X4), scales=x_scales[:],
-                                  in_=xn_grouped[:].rearrange("p r t -> p (r t)"))
-            x_mx[s] = (x_codes, x_scales)
 
-        def turn_h(s):
-            h_sb = h_tiles.pop(s)
-            h_ps = psum_rot.tile([P, HEADS, TILES, P], BF16, tag="turn")
-            for h in range(HEADS):
-                for j in range(TILES):
-                    nc.tensor.transpose(h_ps[:, h, j, :], h_sb[:, j, h * D_HEAD:(h + 1) * D_HEAD],
-                                        ident_bf16[:])
-            h_turned = work.tile([P, HEADS, TILES, P], BF16, tag="h_turned")
-            nc.scalar.copy(out=h_turned[:], in_=h_ps[:])
-            ht_tiles[s] = h_turned
+            def quantise_xn(c):
+                xn_grouped = work.tile([P, CHUNK, PACK], BF16, tag="xn_grouped", bufs=1,
+                                       align_bytes=64)
+                nc.vector.tensor_copy(out=xn_grouped[:],
+                                      in_=planes.pop(c)[:].rearrange("p t r -> p r t"))
+                x_codes = work.tile([P, CHUNK], U32, tag="x_codes", align_bytes=64)
+                x_scales = work.tile([P, CHUNK], U8, tag="x_scales", align_bytes=64)
+                nc.vector.quantize_mx(out=x_codes[:].bitcast(FP8X4), scales=x_scales[:],
+                                      in_=xn_grouped[:].rearrange("p r t -> p (r t)"))
+                x_mx[c] = (x_codes, x_scales)
 
-        def gate_products(s):
-            x_codes, x_scales = x_mx.pop(s)
-            mx_turned = work.tile([P, BLOCKS, CHUNK], F32, tag="mx_turned")
-            for blk in range(BLOCKS):
+            def turn_h(c):
+                h_sb = h_tiles.pop(c)
+                h_ps = psum_rot.tile([P, HEADS, TILES, P], BF16, tag="turn")
+                for h in range(HEADS):
+                    for j in range(TILES):
+                        nc.tensor.transpose(h_ps[:, h, j, :],
+                                            h_sb[:, j, h * D_HEAD:(h + 1) * D_HEAD], ident_bf16[:])
+                h_turned[c] = work.tile([P, HEADS, TILES, P], BF16, tag="h_turned", name="h_turned")
+                nc.scalar.copy(out=h_turned[c][:], in_=h_ps[:])
+
+            def mx_pass(c, blk):
+                x_codes, x_scales = x_mx[c]
                 cols = slice(blk * P, (blk + 1) * P)
                 mx_ps = psum_rot.tile([P, CHUNK], F32, tag="mx_ps")
                 nc.tensor.matmul_mx(out=mx_ps[:],
-                                    lhsT=w_codes[:, cols].bitcast(FP8X4), lhsT_scale=w_scales[:, cols],
+                                    lhsT=w_codes[:, cols].bitcast(FP8X4),
+                                    lhsT_scale=w_scales[:, cols],
                                     rhs=x_codes[:].bitcast(FP8X4), rhs_scale=x_scales[:],
                                     start=True, stop=True)
-                nc.scalar.activation(out=mx_turned[:, blk, :], in_=mx_ps[:], func=ACT.Identity,
+                return mx_ps
+
+            def mx_out(c, blk, mx_ps):
+                nc.scalar.activation(out=mx_turned[c][:, blk, :], in_=mx_ps[:], func=ACT.Identity,
                                      bias=gate_bias[:, blk:blk + 1], scale=1.0)
-            mt_tiles[s] = mx_turned
 
-        m_out = {}
+            def pre_activations(u):
+                c, q = divmod(u, PAIRS)
+                pre[u] = {}
+                for g in (GF, GZ, GO, GI):
+                    pre_g = psum_pre.tile([P, PAIR, D_HID], F32, tag="pre%d" % g, name="pre_g")
+                    for jj in range(PAIR):
+                        j = q * PAIR + jj
+                        for h in range(HEADS):
+                            out = pre_g[:, jj, h * D_HEAD:(h + 1) * D_HEAD]
+                            nc.tensor.matmul(out=out,
+                                             lhsT=mx_turned[c][:, g * HEADS + h, j * P:(j + 1) * P],
+                                             rhs=ident_f32[:], start=True, stop=False,
+                                             is_transpose=True)
+                            nc.tensor.matmul(out=out, lhsT=h_turned[c][:, h, j, :],
+                                             rhs=r_sb[:, g, h, :], start=False, stop=True)
+                    pre[u][g] = pre_g
 
-        def gating(s, q):
-            mx_turned = mt_tiles[s]
-            h_turned = ht_tiles[s]
-            tiles = slice(q * PAIR, (q + 1) * PAIR)
-            pre = []
-            for g in range(GATES):
-                pre_g = psum_pre.tile([P, PAIR, D_HID], F32, tag="pre%d" % g, name="pre_g")
-                for jj in range(PAIR):
-                    j = q * PAIR + jj
-                    for h in range(HEADS):
-                        out = pre_g[:, jj, h * D_HEAD:(h + 1) * D_HEAD]
-                        nc.tensor.matmul(out=out, lhsT=mx_turned[:, g * HEADS + h, j * P:(j + 1) * P],
-                                         rhs=ident_f32[:], start=True, stop=False, is_transpose=True)
-                        nc.tensor.matmul(out=out, lhsT=h_turned[:, h, j, :], rhs=r_sb[:, g, h, :],
-                                         start=False, stop=True)
-                pre.append(pre_g)
-            shape = [P, PAIR, D_HID]
-            zt = work.tile(shape, F32, tag="zt")
-            nc.scalar.activation(out=zt[:], in_=pre[GZ][:], func=ACT.Tanh)
-            nc.scalar.activation(out=th_keep[s][:, tiles, :], in_=pre[GO][:], func=ACT.Tanh, scale=0.5)
-            fm = work.tile(shape, F32, tag="fm")
-            nc.vector.tensor_tensor(out=fm[:], in0=pre[GF][:], in1=m_tiles[s][:, tiles, :], op=ALU.add)
-            diff = work.tile(shape, F32, tag="diff")
-            nc.vector.tensor_tensor(out=diff[:], in0=pre[GI][:], in1=fm[:], op=ALU.subtract)
-            if q == 0:
-                m_out[s] = work.tile([P, TILES, D_HID], F32, tag="out_stage", name="m_stage")
-            nc.vector.tensor_tensor(out=m_out[s][:, tiles, :], in0=pre[GI][:], in1=fm[:], op=ALU.max)
-            e_i = work.tile(shape, F32, tag="e_i")
-            nc.scalar.activation(out=e_i[:], in_=diff[:], func=ACT.Exp)
-            e_f = work.tile(shape, F32, tag="e_f")
-            nc.scalar.activation(out=e_f[:], in_=diff[:], func=ACT.Exp, scale=-1.0)
-            ct = ct_keep[s][:, tiles, :]
-            nt = nt_keep[s][:, tiles, :]
-            iz = work.tile(shape, F32, tag="iz", bufs=1)
-            nc.vector.scalar_tensor_tensor(out=ct, in0=e_f[:], scalar=1.0, in1=c_tiles[s][:, tiles, :],
-                                           op0=ALU.min, op1=ALU.mult)
-            nc.vector.scalar_tensor_tensor(out=nt, in0=e_f[:], scalar=1.0, in1=n_tiles[s][:, tiles, :],
-                                           op0=ALU.min, op1=ALU.mult)
-            nc.vector.scalar_tensor_tensor(out=iz[:], in0=e_i[:], scalar=1.0, in1=zt[:],
-                                           op0=ALU.min, op1=ALU.mult)
-            nc.vector.scalar_tensor_tensor(out=nt, in0=e_i[:], scalar=1.0, in1=nt,
-                                           op0=ALU.min, op1=ALU.add)
-            nc.vector.tensor_tensor(out=ct, in0=ct, in1=iz[:], op=ALU.add)
-
-        def store_chunk(s):
-            nc.sync.dma_start(out=chunk_rows(out_3, s), in_=m_out.pop(s)[:])
-            nc.sync.dma_start(out=chunk_rows(out_2, s), in_=nt_keep[s][:])
-            nc.sync.dma_start(out=chunk_rows(out_1, s), in_=ct_keep[s][:])
-
-        normalise(0)
-        load_x(1)
-        quantise_xn(0)
-        turn_h(0)
-        gate_products(0)
-        for s in range(N_CHUNKS):
-            nxt = s + 1
-            if nxt < N_CHUNKS:
-                normalise(nxt)
-                load_state(nxt)
-            if nxt + 1 < N_CHUNKS:
-                load_x(nxt + 1)
-            gating(s, 0)
-            if nxt < N_CHUNKS:
-                quantise_xn(nxt)
-                turn_h(nxt)
-            gating(s, 1)
-            store_chunk(s)
-            if nxt < N_CHUNKS:
-                gate_products(nxt)
-
-        for s in range(N_CHUNKS):
-            h_stage = work.tile([P, TILES, D_HID], F32, tag="out_stage")
-            for q in range(N_PAIRS):
-                tiles = slice(q * PAIR, (q + 1) * PAIR)
+            def gating(new, old):
                 shape = [P, PAIR, D_HID]
-                rs = work.tile(shape, F32, tag="e_i")
-                nc.scalar.activation(out=rs[:], in_=nt_keep[s][:, tiles, :],
-                                     func=ACT.Abs_reciprocal_sqrt, bias=div_eps[:, 0:1], scale=1.0)
-                rs2 = work.tile(shape, F32, tag="e_f")
-                nc.scalar.activation(out=rs2[:], in_=rs[:], func=ACT.Square)
-                rs4 = work.tile(shape, F32, tag="zt")
-                nc.scalar.activation(out=rs4[:], in_=rs2[:], func=ACT.Square)
-                inv = work.tile(shape, F32, tag="fm")
-                nc.vector.scalar_tensor_tensor(out=inv[:], in0=nt_keep[s][:, tiles, :], scalar=DIV_EPS,
-                                               in1=rs4[:], op0=ALU.add, op1=ALU.mult)
-                quot = work.tile(shape, F32, tag="diff")
-                nc.vector.scalar_tensor_tensor(out=quot[:], in0=ct_keep[s][:, tiles, :], scalar=0.5,
-                                               in1=inv[:], op0=ALU.mult, op1=ALU.mult)
-                nc.vector.scalar_tensor_tensor(out=h_stage[:, tiles, :], in0=th_keep[s][:, tiles, :],
-                                               scalar=1.0, in1=quot[:], op0=ALU.add, op1=ALU.mult)
-            nc.sync.dma_start(out=chunk_rows(out_0, s), in_=h_stage[:])
+                if new is not None:
+                    c, q = divmod(new, PAIRS)
+                    tiles = slice(q * PAIR, (q + 1) * PAIR)
+                    bank = pre.pop(new)
+                    zt = work.tile(shape, F32, tag="zt")
+                    nc.scalar.activation(out=zt[:], in_=bank[GZ][:], func=ACT.Tanh)
+                    nc.scalar.activation(out=th_keep[c][:, tiles, :], in_=bank[GO][:], func=ACT.Tanh,
+                                         scale=0.5)
+                    fm = work.tile(shape, F32, tag="fm", bufs=1)
+                    nc.vector.tensor_tensor(out=fm[:], in0=bank[GF][:], in1=m_tiles[c][:, tiles, :],
+                                            op=ALU.add)
+                if old is not None:
+                    co, qo = divmod(old, PAIRS)
+                    tiles_o = slice(qo * PAIR, (qo + 1) * PAIR)
+                    zt_o, e_i_o, e_f_o = gate_tiles.pop(old)
+                    ct = ct_keep[co][:, tiles_o, :]
+                    nt = nt_keep[co][:, tiles_o, :]
+                    nc.vector.scalar_tensor_tensor(out=ct, in0=e_f_o[:], scalar=1.0,
+                                                   in1=c_tiles[co][:, tiles_o, :],
+                                                   op0=ALU.min, op1=ALU.mult)
+                if new is not None:
+                    diff = work.tile(shape, F32, tag="diff")
+                    nc.vector.tensor_tensor(out=diff[:], in0=bank[GI][:], in1=fm[:], op=ALU.subtract)
+                    e_i = work.tile(shape, F32, tag="e_i")
+                    nc.scalar.activation(out=e_i[:], in_=diff[:], func=ACT.Exp)
+                    e_f = work.tile(shape, F32, tag="e_f")
+                    nc.scalar.activation(out=e_f[:], in_=diff[:], func=ACT.Exp, scale=-1.0)
+                    gate_tiles[new] = (zt, e_i, e_f)
+                if old is not None:
+                    nc.vector.scalar_tensor_tensor(out=nt, in0=e_f_o[:], scalar=1.0,
+                                                   in1=n_tiles[co][:, tiles_o, :],
+                                                   op0=ALU.min, op1=ALU.mult)
+                if new is not None:
+                    if q == 0:
+                        m_stage[c] = work.tile([P, TILES, D_HID], F32, tag="m_stage", name="m_stage")
+                    nc.vector.tensor_tensor(out=m_stage[c][:, tiles, :], in0=bank[GI][:], in1=fm[:],
+                                            op=ALU.max)
+                if old is not None:
+                    iz = work.tile(shape, F32, tag="iz", bufs=1)
+                    nc.vector.scalar_tensor_tensor(out=iz[:], in0=e_i_o[:], scalar=1.0, in1=zt_o[:],
+                                                   op0=ALU.min, op1=ALU.mult)
+                    nc.vector.scalar_tensor_tensor(out=nt, in0=e_i_o[:], scalar=1.0, in1=nt,
+                                                   op0=ALU.min, op1=ALU.add)
+                    nc.vector.tensor_tensor(out=ct, in0=ct, in1=iz[:], op=ALU.add)
+
+            def store_chunk(c):
+                nc.sync.dma_start(out=chunk_rows(out_3, c), in_=m_stage.pop(c)[:])
+                nc.sync.dma_start(out=chunk_rows(out_2, c), in_=nt_keep[c][:])
+                nc.sync.dma_start(out=chunk_rows(out_1, c), in_=ct_keep[c][:])
+
+            def chunk_due(u, lead):
+                c, rest = divmod(u + lead, PAIRS)
+                return c if rest == 0 and 0 <= c < N_CHUNKS else None
+
+            normalise(0)
+
+            with tc.tile_pool(name="setup", bufs=2) as setup:
+                w_raw = []
+                for g in range(GATES):
+                    w_raw.append(setup.tile([P, PACK, D_HID], BF16, name="w_raw", bufs=GATES))
+                    nc.sync.dma_start(out=w_raw[g][:],
+                                      in_=weights[g].rearrange("(t p) f -> p t f", p=P))
+                load_x(1)
+                load_h(0)
+                for g in range(GATES):
+                    nc.sync.dma_start(out=r_sb[:, g, :, :],
+                                      in_=recurrents[g].rearrange("h k f -> k h f"))
+                load_x(2)
+                vec_ps = psum_rot.tile([P, P], BF16, tag="turn")
+                nc.tensor.transpose(vec_ps[:], vec_rows[:], ident_bf16[:])
+                nc.vector.tensor_copy(out=vec_cols[:], in_=vec_ps[:, 0:24])
+                nc.vector.tensor_add(out=gate_bias[:], in0=vec_cols[:, 8:16], in1=vec_cols[:, 16:24])
+                for g in range(GATES):
+                    w_grouped = setup.tile([P, D_HID, PACK], BF16, align_bytes=64)
+                    nc.scalar.copy(out=w_grouped[:], in_=w_raw[g][:].rearrange("p t f -> p f t"))
+                    cols = slice(g * D_HID, (g + 1) * D_HID)
+                    nc.vector.quantize_mx(out=w_codes[:, cols].bitcast(FP8X4),
+                                          scales=w_scales[:, cols],
+                                          in_=w_grouped[:].rearrange("p f t -> p (f t)"))
+            products = main_stack.enter_context(
+                tc.tile_pool(name="products", bufs=2, reuse_waits="tile"))
+
+            for u in range(-6, N_PAIRS + 1):
+                c = chunk_due(u, 11)
+                if c is not None and c >= 3:
+                    load_x(c)
+                c = chunk_due(u, 6)
+                if c is not None and c >= 1:
+                    load_h(c)
+
+                c_mx, half = chunk_due(u, 3), 0
+                if c_mx is None:
+                    c_mx, half = chunk_due(u, 2), 1
+                c_ln, t0 = chunk_due(u, 6), 0
+                if c_ln is None:
+                    c_ln, t0 = chunk_due(u, 5), 2
+                blk0 = half * (BLOCKS // 2)
+
+                if c_mx is not None:
+                    if half == 0:
+                        mx_turned[c_mx] = products.tile([P, BLOCKS, CHUNK], F32, name="mx_turned")
+                    bank_a = mx_pass(c_mx, blk0)
+                    bank_b = mx_pass(c_mx, blk0 + 1)
+                if c_ln is not None:
+                    turned_a = turn_xn(c_ln, t0)
+                    turned_b = turn_xn(c_ln, t0 + 1)
+                gating(u if 0 <= u < N_PAIRS else None, u - 1 if u >= 1 else None)
+                if 0 <= u + 1 < N_PAIRS:
+                    pre_activations(u + 1)
+                if c_mx is not None:
+                    mx_out(c_mx, blk0, bank_a)
+                    mx_out(c_mx, blk0 + 1, bank_b)
+                if c_ln is not None:
+                    scale_xn(c_ln, t0, turned_a)
+                    scale_xn(c_ln, t0 + 1, turned_b)
+                if c_mx is not None:
+                    bank_a = mx_pass(c_mx, blk0 + 2)
+                    bank_b = mx_pass(c_mx, blk0 + 3)
+                    mx_out(c_mx, blk0 + 2, bank_a)
+                    mx_out(c_mx, blk0 + 3, bank_b)
+                    if half == 0:
+                        turn_h(c_mx)
+
+                c = chunk_due(u, 4)
+                if c is not None:
+                    quantise_xn(c)
+                c = chunk_due(u, 7)
+                if c is not None:
+                    normalise(c)
+                c = chunk_due(u, 2)
+                if c is not None:
+                    load_state(c)
+                c = chunk_due(u, -2)
+                if c is not None:
+                    store_chunk(c)
+
+        with tc.tile_pool(name="tail", bufs=3, reuse_waits="tile") as tail:
+            halves = [slice(q * PAIR, (q + 1) * PAIR) for q in range(PAIRS)]
+            for c in range(N_CHUNKS):
+                inv = tail.tile([P, TILES, D_HID], F32)
+                h_stage = tail.tile([P, TILES, D_HID], F32)
+                for tiles in halves:
+                    nc.scalar.activation(out=inv[:, tiles, :], in_=nt_keep[c][:, tiles, :],
+                                         func=ACT.Abs_reciprocal_sqrt, bias=div_eps[:, 0:1], scale=1.0)
+                for tiles in halves:
+                    nc.scalar.activation(out=inv[:, tiles, :], in_=inv[:, tiles, :], func=ACT.Square)
+                for tiles in halves:
+                    nc.scalar.activation(out=inv[:, tiles, :], in_=inv[:, tiles, :], func=ACT.Square)
+                for tiles in halves:
+                    nc.vector.scalar_tensor_tensor(out=inv[:, tiles, :], in0=nt_keep[c][:, tiles, :],
+                                                   scalar=DIV_EPS, in1=inv[:, tiles, :],
+                                                   op0=ALU.add, op1=ALU.mult)
+                for tiles in halves:
+                    nc.vector.scalar_tensor_tensor(out=inv[:, tiles, :], in0=ct_keep[c][:, tiles, :],
+                                                   scalar=0.5, in1=inv[:, tiles, :],
+                                                   op0=ALU.mult, op1=ALU.mult)
+                for tiles in halves:
+                    nc.vector.scalar_tensor_tensor(out=h_stage[:, tiles, :],
+                                                   in0=th_keep[c][:, tiles, :], scalar=1.0,
+                                                   in1=inv[:, tiles, :], op0=ALU.add, op1=ALU.mult)
+                nc.sync.dma_start(out=chunk_rows(out_0, c), in_=h_stage[:])

@@ -27,8 +27,7 @@ TILES = 4
 CHUNK = TILES * P
 N_CHUNKS = ROWS // CHUNK
 PAIR = 2
-PAIRS = TILES // PAIR
-N_PAIRS = ROWS // (PAIR * P)
+N_PAIRS = TILES // PAIR
 
 FLOPS = 2 * ROWS * D_IN * GATES * D_HID + 2 * ROWS * D_HEAD * GATES * D_HID
 
@@ -49,45 +48,12 @@ def tile_slstmblock_pa_t_kernel(
         return dram[s * CHUNK:(s + 1) * CHUNK, :].rearrange("(p j) w -> p j w", j=TILES)
 
     with ExitStack() as stack:
-        stack.enter_context(tc.manual_schedule())
         const = stack.enter_context(tc.tile_pool(name="const", bufs=1))
         keep = stack.enter_context(tc.tile_pool(name="keep", bufs=1))
         loads = stack.enter_context(tc.tile_pool(name="loads", bufs=2))
         psum_pre = stack.enter_context(tc.psum_pool(name="psum_pre", bufs=1))
         psum_rot = stack.enter_context(tc.psum_pool(name="psum_rot", bufs=2))
 
-        x_tiles = {}
-        h_tiles = {}
-        c_tiles = {}
-        n_tiles = {}
-        m_tiles = {}
-
-        def load_x(c):
-            x_tiles[c] = loads.tile([P, TILES, D_IN], BF16, tag="x_sb", name="x_sb", bufs=3)
-            nc.sync.dma_start(out=x_tiles[c][:], in_=chunk_rows(x, c))
-
-        def load_h(c):
-            h_tiles[c] = loads.tile([P, TILES, D_HID], BF16, tag="h_sb", name="h_sb")
-            nc.sync.dma_start(out=h_tiles[c][:], in_=chunk_rows(h_prev, c))
-
-        def load_state(c):
-            m_tiles[c] = loads.tile([P, TILES, D_HID], BF16, tag="m_sb", name="m_sb")
-            nc.sync.dma_start(out=m_tiles[c][:], in_=chunk_rows(m_prev, c))
-            c_tiles[c] = loads.tile([P, TILES, D_HID], BF16, tag="c_sb", name="c_sb")
-            nc.sync.dma_start(out=c_tiles[c][:], in_=chunk_rows(c_prev, c))
-            n_tiles[c] = loads.tile([P, TILES, D_HID], BF16, tag="n_sb", name="n_sb")
-            nc.sync.dma_start(out=n_tiles[c][:], in_=chunk_rows(n_prev, c))
-
-        load_x(0)
-        vec_rows = const.tile([P, P], BF16)
-        nc.vector.memset(vec_rows[:], 0.0)
-        nc.scalar.dma_start(out=vec_rows[0:4, :], in_=ln_w.rearrange("(t p) -> t p", p=P))
-        nc.scalar.dma_start(out=vec_rows[4:8, :], in_=ln_b.rearrange("(t p) -> t p", p=P))
-        for g in range(GATES):
-            nc.scalar.dma_start(out=vec_rows[8 + HEADS * g:8 + HEADS * (g + 1), :],
-                                in_=biases[g].rearrange("(h f) -> h f", f=D_HEAD))
-            nc.scalar.dma_start(out=vec_rows[16 + HEADS * g:16 + HEADS * (g + 1), :],
-                                in_=rec_biases[g].rearrange("(h f) -> h f", f=D_HEAD))
         ident_f32 = const.tile([P, P], F32)
         make_identity(nc, ident_f32[:])
         ident_bf16 = const.tile([P, P], BF16)
@@ -97,31 +63,90 @@ def tile_slstmblock_pa_t_kernel(
         div_eps = const.tile([P, 1], F32)
         nc.vector.memset(div_eps[:], DIV_EPS)
 
+        vec_rows = const.tile([P, P], BF16)
+        nc.vector.memset(vec_rows[:], 0.0)
+        nc.scalar.dma_start(out=vec_rows[0:4, :], in_=ln_w.rearrange("(t p) -> t p", p=P))
+        nc.scalar.dma_start(out=vec_rows[4:8, :], in_=ln_b.rearrange("(t p) -> t p", p=P))
+        for g in range(GATES):
+            nc.scalar.dma_start(out=vec_rows[8 + HEADS * g:8 + HEADS * (g + 1), :],
+                                in_=biases[g].rearrange("(h f) -> h f", f=D_HEAD))
+            nc.scalar.dma_start(out=vec_rows[16 + HEADS * g:16 + HEADS * (g + 1), :],
+                                in_=rec_biases[g].rearrange("(h f) -> h f", f=D_HEAD))
+
+        x_tiles = {}
+        h_tiles = {}
+        c_tiles = {}
+        n_tiles = {}
+        m_tiles = {}
+
+        def load_x(s):
+            x_sb = loads.tile([P, TILES, D_IN], BF16, tag="x_sb", bufs=3)
+            nc.sync.dma_start(out=x_sb[:], in_=chunk_rows(x, s))
+            x_tiles[s] = x_sb
+
+        def load_state(s):
+            h_sb = loads.tile([P, TILES, D_HID], BF16, tag="h_sb")
+            nc.sync.dma_start(out=h_sb[:], in_=chunk_rows(h_prev, s))
+            h_tiles[s] = h_sb
+            m_sb = loads.tile([P, TILES, D_HID], BF16, tag="m_sb")
+            nc.sync.dma_start(out=m_sb[:], in_=chunk_rows(m_prev, s))
+            m_tiles[s] = m_sb
+            c_sb = loads.tile([P, TILES, D_HID], BF16, tag="c_sb")
+            nc.sync.dma_start(out=c_sb[:], in_=chunk_rows(c_prev, s))
+            c_tiles[s] = c_sb
+            n_sb = loads.tile([P, TILES, D_HID], BF16, tag="n_sb")
+            nc.sync.dma_start(out=n_sb[:], in_=chunk_rows(n_prev, s))
+            n_tiles[s] = n_sb
+
+        load_x(0)
+
         w_codes = const.tile([P, GATES * D_HID], U32, align_bytes=64)
         w_scales = const.tile([P, GATES * D_HID], U8, align_bytes=64)
         r_sb = const.tile([P, GATES, HEADS, D_HEAD], BF16)
+        with tc.tile_pool(name="setup", bufs=2) as setup:
+            for g in range(GATES):
+                w_raw = setup.tile([P, PACK, D_HID], BF16)
+                nc.sync.dma_start(out=w_raw[:], in_=weights[g].rearrange("(t p) f -> p t f", p=P))
+                w_grouped = setup.tile([P, D_HID, PACK], BF16, align_bytes=64)
+                nc.scalar.copy(out=w_grouped[:], in_=w_raw[:].rearrange("p t f -> p f t"))
+                cols = slice(g * D_HID, (g + 1) * D_HID)
+                nc.vector.quantize_mx(
+                    out=w_codes[:, cols].bitcast(FP8X4),
+                    scales=w_scales[:, cols],
+                    in_=w_grouped[:].rearrange("p f t -> p (f t)"),
+                )
+        load_x(1)
+        load_state(0)
+        for g in range(GATES):
+            nc.sync.dma_start(out=r_sb[:, g, :, :], in_=recurrents[g].rearrange("h k f -> k h f"))
+        load_x(2)
+
+        vec_ps = psum_rot.tile([P, P], BF16, tag="turn")
+        nc.tensor.transpose(vec_ps[:], vec_rows[:], ident_bf16[:])
         vec_cols = const.tile([P, 24], F32)
+        nc.vector.tensor_copy(out=vec_cols[:], in_=vec_ps[:, 0:24])
         gain = vec_cols[:, 0:4]
         shift = vec_cols[:, 4:8]
         gate_bias = const.tile([P, BLOCKS], F32)
+        nc.vector.tensor_add(out=gate_bias[:], in0=vec_cols[:, 8:16], in1=vec_cols[:, 16:24])
 
-        ct_keep = [keep.tile([P, TILES, D_HID], F32, name="ct_keep%d" % c) for c in range(N_CHUNKS)]
-        nt_keep = [keep.tile([P, TILES, D_HID], F32, name="nt_keep%d" % c) for c in range(N_CHUNKS)]
-        th_keep = [keep.tile([P, TILES, D_HID], F32, name="th_keep%d" % c) for c in range(N_CHUNKS)]
+        nt_keep = [keep.tile([P, TILES, D_HID], F32, name="nt_keep%d" % s) for s in range(N_CHUNKS)]
+        oc_keep = [keep.tile([P, TILES, D_HID], F32, name="oc_keep%d" % s) for s in range(N_CHUNKS)]
+        sg_keep = [keep.tile([P, TILES, D_HID], BF16, name="sg_keep%d" % s) for s in range(N_CHUNKS)]
 
         with ExitStack() as main_stack:
-            work = main_stack.enter_context(tc.tile_pool(name="work", bufs=2))
+            products = main_stack.enter_context(
+                tc.tile_pool(name="products", bufs=2, reuse_waits="tile"))
+            work = main_stack.enter_context(tc.tile_pool(name="work", bufs=2, reuse_waits="tile"))
             xh_tiles = {}
-            planes = {}
             x_mx = {}
-            h_turned = {}
-            mx_turned = {}
-            pre = {}
-            gate_tiles = {}
-            m_stage = {}
+            ht_tiles = {}
+            mt_tiles = {}
+            m_out = {}
+            c_out = {}
 
-            def normalise(c):
-                x_sb = x_tiles.pop(c)
+            def normalise(s):
+                x_sb = x_tiles.pop(s)
                 stats = work.tile([P, TILES, 6], F32, tag="stats")
                 mean_var = work.tile([P, TILES, 2], F32, tag="mean_var")
                 for j in range(TILES):
@@ -134,240 +159,157 @@ def tile_slstmblock_pa_t_kernel(
                 nc.vector.tensor_scalar_mul(out=neg_mean[:], in0=mean_var[:, :, 0], scalar1=-1.0)
                 rstd = work.tile([P, TILES], F32, tag="rstd")
                 nc.gpsimd.tensor_tensor(out=rstd[:], in0=var_eps[:], in1=neg_half[:], op=ALU.pow)
-                xh_tiles[c] = []
+                xh = []
                 for j in range(TILES):
                     xh_j = work.tile([P, D_IN], F32, tag="xh", bufs=2 * TILES)
                     nc.gpsimd.tensor_scalar(out=xh_j[:], in0=x_sb[:, j, :],
                                             scalar1=neg_mean[:, j:j + 1], scalar2=rstd[:, j:j + 1],
                                             op0=ALU.add, op1=ALU.mult)
-                    xh_tiles[c].append(xh_j)
+                    xh.append(xh_j)
+                xh_tiles[s] = xh
 
-            def turn_xn(c, t):
-                turned = psum_rot.tile([P, CHUNK], F32, tag="turn")
-                for j in range(TILES):
-                    nc.tensor.transpose(turned[:, j * P:(j + 1) * P],
-                                        xh_tiles[c][j][:, t * P:(t + 1) * P], ident_f32[:])
-                return turned
-
-            def scale_xn(c, t, turned):
-                if t == 0:
-                    planes[c] = work.tile([P, PACK, CHUNK], BF16, tag="xn_planes", name="xn_planes")
-                nc.scalar.activation(out=planes[c][:, t, :], in_=turned[:], func=ACT.Identity,
-                                     bias=shift[:, t:t + 1], scale=gain[:, t:t + 1])
-
-            def quantise_xn(c):
+            def quantise_xn(s):
+                xh = xh_tiles.pop(s)
+                xn_planes = work.tile([P, PACK, CHUNK], BF16, tag="xn_planes", bufs=1)
+                for t in range(PACK):
+                    turned = psum_rot.tile([P, CHUNK], F32, tag="turn")
+                    for j in range(TILES):
+                        nc.tensor.transpose(turned[:, j * P:(j + 1) * P],
+                                            xh[j][:, t * P:(t + 1) * P], ident_f32[:])
+                    nc.scalar.activation(out=xn_planes[:, t, :], in_=turned[:], func=ACT.Identity,
+                                         bias=shift[:, t:t + 1], scale=gain[:, t:t + 1])
                 xn_grouped = work.tile([P, CHUNK, PACK], BF16, tag="xn_grouped", bufs=1,
                                        align_bytes=64)
-                nc.vector.tensor_copy(out=xn_grouped[:],
-                                      in_=planes.pop(c)[:].rearrange("p t r -> p r t"))
-                x_codes = work.tile([P, CHUNK], U32, tag="x_codes", align_bytes=64)
-                x_scales = work.tile([P, CHUNK], U8, tag="x_scales", align_bytes=64)
+                nc.vector.tensor_copy(out=xn_grouped[:].rearrange("p (c i) t -> p c t i", i=4),
+                                      in_=xn_planes[:].rearrange("p t (c i) -> p c t i", i=4))
+                x_codes = work.tile([P, CHUNK], U32, tag="x_codes", bufs=3, align_bytes=64)
+                x_scales = work.tile([P, CHUNK], U8, tag="x_scales", bufs=3, align_bytes=64)
                 nc.vector.quantize_mx(out=x_codes[:].bitcast(FP8X4), scales=x_scales[:],
                                       in_=xn_grouped[:].rearrange("p r t -> p (r t)"))
-                x_mx[c] = (x_codes, x_scales)
+                x_mx[s] = (x_codes, x_scales)
 
-            def turn_h(c):
-                h_sb = h_tiles.pop(c)
+            def turn_h(s):
+                h_sb = h_tiles.pop(s)
                 h_ps = psum_rot.tile([P, HEADS, TILES, P], BF16, tag="turn")
                 for h in range(HEADS):
                     for j in range(TILES):
                         nc.tensor.transpose(h_ps[:, h, j, :],
                                             h_sb[:, j, h * D_HEAD:(h + 1) * D_HEAD], ident_bf16[:])
-                h_turned[c] = work.tile([P, HEADS, TILES, P], BF16, tag="h_turned", name="h_turned")
-                nc.scalar.copy(out=h_turned[c][:], in_=h_ps[:])
+                h_turned = work.tile([P, HEADS, TILES, P], BF16, tag="h_turned")
+                nc.scalar.copy(out=h_turned[:], in_=h_ps[:])
+                ht_tiles[s] = h_turned
 
-            def mx_pass(c, blk):
-                x_codes, x_scales = x_mx[c]
-                cols = slice(blk * P, (blk + 1) * P)
-                mx_ps = psum_rot.tile([P, CHUNK], F32, tag="mx_ps")
-                nc.tensor.matmul_mx(out=mx_ps[:],
-                                    lhsT=w_codes[:, cols].bitcast(FP8X4),
-                                    lhsT_scale=w_scales[:, cols],
-                                    rhs=x_codes[:].bitcast(FP8X4), rhs_scale=x_scales[:],
-                                    start=True, stop=True)
-                return mx_ps
+            def gate_products(s):
+                x_codes, x_scales = x_mx.pop(s)
+                mx_turned = products.tile([P, BLOCKS, CHUNK], F32, tag="mx_turned")
+                for blk in range(BLOCKS):
+                    cols = slice(blk * P, (blk + 1) * P)
+                    mx_ps = psum_rot.tile([P, CHUNK], F32, tag="mx_ps")
+                    nc.tensor.matmul_mx(out=mx_ps[:],
+                                        lhsT=w_codes[:, cols].bitcast(FP8X4),
+                                        lhsT_scale=w_scales[:, cols],
+                                        rhs=x_codes[:].bitcast(FP8X4), rhs_scale=x_scales[:],
+                                        start=True, stop=True)
+                    nc.scalar.activation(out=mx_turned[:, blk, :], in_=mx_ps[:], func=ACT.Identity,
+                                         bias=gate_bias[:, blk:blk + 1], scale=1.0)
+                mt_tiles[s] = mx_turned
 
-            def mx_out(c, blk, mx_ps):
-                nc.scalar.activation(out=mx_turned[c][:, blk, :], in_=mx_ps[:], func=ACT.Identity,
-                                     bias=gate_bias[:, blk:blk + 1], scale=1.0)
-
-            def pre_activations(u):
-                c, q = divmod(u, PAIRS)
-                pre[u] = {}
-                for g in (GF, GZ, GO, GI):
+            def gating(s, q):
+                mx_turned = mt_tiles[s]
+                h_turned = ht_tiles[s]
+                tiles = slice(q * PAIR, (q + 1) * PAIR)
+                pre = []
+                for g in range(GATES):
                     pre_g = psum_pre.tile([P, PAIR, D_HID], F32, tag="pre%d" % g, name="pre_g")
                     for jj in range(PAIR):
                         j = q * PAIR + jj
                         for h in range(HEADS):
                             out = pre_g[:, jj, h * D_HEAD:(h + 1) * D_HEAD]
                             nc.tensor.matmul(out=out,
-                                             lhsT=mx_turned[c][:, g * HEADS + h, j * P:(j + 1) * P],
+                                             lhsT=mx_turned[:, g * HEADS + h, j * P:(j + 1) * P],
                                              rhs=ident_f32[:], start=True, stop=False,
                                              is_transpose=True)
-                            nc.tensor.matmul(out=out, lhsT=h_turned[c][:, h, j, :],
+                            nc.tensor.matmul(out=out, lhsT=h_turned[:, h, j, :],
                                              rhs=r_sb[:, g, h, :], start=False, stop=True)
-                    pre[u][g] = pre_g
-
-            def gating(new, old):
+                    pre.append(pre_g)
                 shape = [P, PAIR, D_HID]
-                if new is not None:
-                    c, q = divmod(new, PAIRS)
-                    tiles = slice(q * PAIR, (q + 1) * PAIR)
-                    bank = pre.pop(new)
-                    zt = work.tile(shape, F32, tag="zt")
-                    nc.scalar.activation(out=zt[:], in_=bank[GZ][:], func=ACT.Tanh)
-                    nc.scalar.activation(out=th_keep[c][:, tiles, :], in_=bank[GO][:], func=ACT.Tanh,
-                                         scale=0.5)
-                    fm = work.tile(shape, F32, tag="fm", bufs=1)
-                    nc.vector.tensor_tensor(out=fm[:], in0=bank[GF][:], in1=m_tiles[c][:, tiles, :],
-                                            op=ALU.add)
-                if old is not None:
-                    co, qo = divmod(old, PAIRS)
-                    tiles_o = slice(qo * PAIR, (qo + 1) * PAIR)
-                    zt_o, e_i_o, e_f_o = gate_tiles.pop(old)
-                    ct = ct_keep[co][:, tiles_o, :]
-                    nt = nt_keep[co][:, tiles_o, :]
-                    nc.vector.scalar_tensor_tensor(out=ct, in0=e_f_o[:], scalar=1.0,
-                                                   in1=c_tiles[co][:, tiles_o, :],
-                                                   op0=ALU.min, op1=ALU.mult)
-                if new is not None:
-                    diff = work.tile(shape, F32, tag="diff")
-                    nc.vector.tensor_tensor(out=diff[:], in0=bank[GI][:], in1=fm[:], op=ALU.subtract)
-                    e_i = work.tile(shape, F32, tag="e_i")
-                    nc.scalar.activation(out=e_i[:], in_=diff[:], func=ACT.Exp)
-                    e_f = work.tile(shape, F32, tag="e_f")
-                    nc.scalar.activation(out=e_f[:], in_=diff[:], func=ACT.Exp, scale=-1.0)
-                    gate_tiles[new] = (zt, e_i, e_f)
-                if old is not None:
-                    nc.vector.scalar_tensor_tensor(out=nt, in0=e_f_o[:], scalar=1.0,
-                                                   in1=n_tiles[co][:, tiles_o, :],
-                                                   op0=ALU.min, op1=ALU.mult)
-                if new is not None:
-                    if q == 0:
-                        m_stage[c] = work.tile([P, TILES, D_HID], F32, tag="m_stage", name="m_stage")
-                    nc.vector.tensor_tensor(out=m_stage[c][:, tiles, :], in0=bank[GI][:], in1=fm[:],
-                                            op=ALU.max)
-                if old is not None:
-                    iz = work.tile(shape, F32, tag="iz", bufs=1)
-                    nc.vector.scalar_tensor_tensor(out=iz[:], in0=e_i_o[:], scalar=1.0, in1=zt_o[:],
-                                                   op0=ALU.min, op1=ALU.mult)
-                    nc.vector.scalar_tensor_tensor(out=nt, in0=e_i_o[:], scalar=1.0, in1=nt,
-                                                   op0=ALU.min, op1=ALU.add)
-                    nc.vector.tensor_tensor(out=ct, in0=ct, in1=iz[:], op=ALU.add)
+                zt = work.tile(shape, F32, tag="zt")
+                nc.scalar.activation(out=zt[:], in_=pre[GZ][:], func=ACT.Tanh)
+                th = work.tile(shape, F32, tag="th")
+                nc.scalar.activation(out=th[:], in_=pre[GO][:], func=ACT.Tanh, scale=0.5)
+                fm = work.tile(shape, F32, tag="fm")
+                nc.vector.tensor_tensor(out=fm[:], in0=pre[GF][:], in1=m_tiles[s][:, tiles, :],
+                                        op=ALU.add)
+                diff = work.tile(shape, F32, tag="diff")
+                nc.vector.tensor_tensor(out=diff[:], in0=pre[GI][:], in1=fm[:], op=ALU.subtract)
+                if q == 0:
+                    m_out[s] = work.tile([P, TILES, D_HID], F32, tag="m_stage", name="m_stage")
+                    c_out[s] = work.tile([P, TILES, D_HID], F32, tag="c_stage", name="c_stage")
+                nc.vector.tensor_tensor(out=m_out[s][:, tiles, :], in0=pre[GI][:], in1=fm[:],
+                                        op=ALU.max)
+                e_i = work.tile(shape, F32, tag="e_i")
+                nc.scalar.activation(out=e_i[:], in_=diff[:], func=ACT.Exp)
+                e_f = work.tile(shape, F32, tag="e_f")
+                nc.scalar.activation(out=e_f[:], in_=diff[:], func=ACT.Exp, scale=-1.0)
+                ct = c_out[s][:, tiles, :]
+                nt = nt_keep[s][:, tiles, :]
+                iz = work.tile(shape, F32, tag="iz", bufs=1)
+                nc.vector.scalar_tensor_tensor(out=ct, in0=e_f[:], scalar=1.0,
+                                               in1=c_tiles[s][:, tiles, :],
+                                               op0=ALU.min, op1=ALU.mult)
+                nc.vector.scalar_tensor_tensor(out=nt, in0=e_f[:], scalar=1.0,
+                                               in1=n_tiles[s][:, tiles, :],
+                                               op0=ALU.min, op1=ALU.mult)
+                nc.vector.scalar_tensor_tensor(out=iz[:], in0=e_i[:], scalar=1.0, in1=zt[:],
+                                               op0=ALU.min, op1=ALU.mult)
+                nc.vector.scalar_tensor_tensor(out=nt, in0=e_i[:], scalar=1.0, in1=nt,
+                                               op0=ALU.min, op1=ALU.add)
+                nc.vector.tensor_tensor(out=ct, in0=ct, in1=iz[:], op=ALU.add)
+                nc.scalar.activation(out=sg_keep[s][:, tiles, :], in_=nt, func=ACT.Sign,
+                                     bias=div_eps[:, 0:1], scale=1.0)
+                nc.vector.scalar_tensor_tensor(out=oc_keep[s][:, tiles, :], in0=th[:], scalar=1.0,
+                                               in1=ct, op0=ALU.add, op1=ALU.mult)
 
-            def store_chunk(c):
-                nc.sync.dma_start(out=chunk_rows(out_3, c), in_=m_stage.pop(c)[:])
-                nc.sync.dma_start(out=chunk_rows(out_2, c), in_=nt_keep[c][:])
-                nc.sync.dma_start(out=chunk_rows(out_1, c), in_=ct_keep[c][:])
-
-            def chunk_due(u, lead):
-                c, rest = divmod(u + lead, PAIRS)
-                return c if rest == 0 and 0 <= c < N_CHUNKS else None
+            def store_chunk(s):
+                nc.sync.dma_start(out=chunk_rows(out_3, s), in_=m_out.pop(s)[:])
+                nc.sync.dma_start(out=chunk_rows(out_2, s), in_=nt_keep[s][:])
+                nc.sync.dma_start(out=chunk_rows(out_1, s), in_=c_out.pop(s)[:])
 
             normalise(0)
-
-            with tc.tile_pool(name="setup", bufs=2) as setup:
-                w_raw = []
-                for g in range(GATES):
-                    w_raw.append(setup.tile([P, PACK, D_HID], BF16, name="w_raw", bufs=GATES))
-                    nc.sync.dma_start(out=w_raw[g][:],
-                                      in_=weights[g].rearrange("(t p) f -> p t f", p=P))
-                load_x(1)
-                load_h(0)
-                for g in range(GATES):
-                    nc.sync.dma_start(out=r_sb[:, g, :, :],
-                                      in_=recurrents[g].rearrange("h k f -> k h f"))
-                load_x(2)
-                vec_ps = psum_rot.tile([P, P], BF16, tag="turn")
-                nc.tensor.transpose(vec_ps[:], vec_rows[:], ident_bf16[:])
-                nc.vector.tensor_copy(out=vec_cols[:], in_=vec_ps[:, 0:24])
-                nc.vector.tensor_add(out=gate_bias[:], in0=vec_cols[:, 8:16], in1=vec_cols[:, 16:24])
-                for g in range(GATES):
-                    w_grouped = setup.tile([P, D_HID, PACK], BF16, align_bytes=64)
-                    nc.scalar.copy(out=w_grouped[:], in_=w_raw[g][:].rearrange("p t f -> p f t"))
-                    cols = slice(g * D_HID, (g + 1) * D_HID)
-                    nc.vector.quantize_mx(out=w_codes[:, cols].bitcast(FP8X4),
-                                          scales=w_scales[:, cols],
-                                          in_=w_grouped[:].rearrange("p f t -> p (f t)"))
-            products = main_stack.enter_context(
-                tc.tile_pool(name="products", bufs=2, reuse_waits="tile"))
-
-            for u in range(-6, N_PAIRS + 1):
-                c = chunk_due(u, 11)
-                if c is not None and c >= 3:
-                    load_x(c)
-                c = chunk_due(u, 6)
-                if c is not None and c >= 1:
-                    load_h(c)
-
-                c_mx, half = chunk_due(u, 3), 0
-                if c_mx is None:
-                    c_mx, half = chunk_due(u, 2), 1
-                c_ln, t0 = chunk_due(u, 6), 0
-                if c_ln is None:
-                    c_ln, t0 = chunk_due(u, 5), 2
-                blk0 = half * (BLOCKS // 2)
-
-                if c_mx is not None:
-                    if half == 0:
-                        mx_turned[c_mx] = products.tile([P, BLOCKS, CHUNK], F32, name="mx_turned")
-                    bank_a = mx_pass(c_mx, blk0)
-                    bank_b = mx_pass(c_mx, blk0 + 1)
-                if c_ln is not None:
-                    turned_a = turn_xn(c_ln, t0)
-                    turned_b = turn_xn(c_ln, t0 + 1)
-                gating(u if 0 <= u < N_PAIRS else None, u - 1 if u >= 1 else None)
-                if 0 <= u + 1 < N_PAIRS:
-                    pre_activations(u + 1)
-                if c_mx is not None:
-                    mx_out(c_mx, blk0, bank_a)
-                    mx_out(c_mx, blk0 + 1, bank_b)
-                if c_ln is not None:
-                    scale_xn(c_ln, t0, turned_a)
-                    scale_xn(c_ln, t0 + 1, turned_b)
-                if c_mx is not None:
-                    bank_a = mx_pass(c_mx, blk0 + 2)
-                    bank_b = mx_pass(c_mx, blk0 + 3)
-                    mx_out(c_mx, blk0 + 2, bank_a)
-                    mx_out(c_mx, blk0 + 3, bank_b)
-                    if half == 0:
-                        turn_h(c_mx)
-
-                c = chunk_due(u, 4)
-                if c is not None:
-                    quantise_xn(c)
-                c = chunk_due(u, 7)
-                if c is not None:
-                    normalise(c)
-                c = chunk_due(u, 2)
-                if c is not None:
-                    load_state(c)
-                c = chunk_due(u, -2)
-                if c is not None:
-                    store_chunk(c)
+            normalise(1)
+            quantise_xn(0)
+            turn_h(0)
+            gate_products(0)
+            for s in range(N_CHUNKS):
+                if s + 3 < N_CHUNKS:
+                    load_x(s + 3)
+                if s + 1 < N_CHUNKS:
+                    load_state(s + 1)
+                if s + 2 < N_CHUNKS:
+                    normalise(s + 2)
+                if s + 1 < N_CHUNKS:
+                    quantise_xn(s + 1)
+                    turn_h(s + 1)
+                    gate_products(s + 1)
+                gating(s, 0)
+                gating(s, 1)
+                store_chunk(s)
 
         with tc.tile_pool(name="tail", bufs=3, reuse_waits="tile") as tail:
-            halves = [slice(q * PAIR, (q + 1) * PAIR) for q in range(PAIRS)]
-            for c in range(N_CHUNKS):
+            halves = [slice(q * PAIR, (q + 1) * PAIR) for q in range(N_PAIRS)]
+            for s in range(N_CHUNKS):
                 inv = tail.tile([P, TILES, D_HID], F32)
                 h_stage = tail.tile([P, TILES, D_HID], F32)
                 for tiles in halves:
-                    nc.scalar.activation(out=inv[:, tiles, :], in_=nt_keep[c][:, tiles, :],
+                    nc.scalar.activation(out=inv[:, tiles, :], in_=nt_keep[s][:, tiles, :],
                                          func=ACT.Abs_reciprocal_sqrt, bias=div_eps[:, 0:1], scale=1.0)
                 for tiles in halves:
                     nc.scalar.activation(out=inv[:, tiles, :], in_=inv[:, tiles, :], func=ACT.Square)
                 for tiles in halves:
-                    nc.scalar.activation(out=inv[:, tiles, :], in_=inv[:, tiles, :], func=ACT.Square)
-                for tiles in halves:
-                    nc.vector.scalar_tensor_tensor(out=inv[:, tiles, :], in0=nt_keep[c][:, tiles, :],
-                                                   scalar=DIV_EPS, in1=inv[:, tiles, :],
-                                                   op0=ALU.add, op1=ALU.mult)
-                for tiles in halves:
-                    nc.vector.scalar_tensor_tensor(out=inv[:, tiles, :], in0=ct_keep[c][:, tiles, :],
+                    nc.vector.scalar_tensor_tensor(out=inv[:, tiles, :], in0=oc_keep[s][:, tiles, :],
                                                    scalar=0.5, in1=inv[:, tiles, :],
                                                    op0=ALU.mult, op1=ALU.mult)
                 for tiles in halves:
-                    nc.vector.scalar_tensor_tensor(out=h_stage[:, tiles, :],
-                                                   in0=th_keep[c][:, tiles, :], scalar=1.0,
-                                                   in1=inv[:, tiles, :], op0=ALU.add, op1=ALU.mult)
-                nc.sync.dma_start(out=chunk_rows(out_0, c), in_=h_stage[:])
+                    nc.vector.tensor_tensor(out=h_stage[:, tiles, :], in0=inv[:, tiles, :],
+                                            in1=sg_keep[s][:, tiles, :], op=ALU.mult)
+                nc.sync.dma_start(out=chunk_rows(out_0, s), in_=h_stage[:])

@@ -28,6 +28,7 @@ CHUNK = TILES * P
 N_CHUNKS = ROWS // CHUNK
 PAIR = 2
 N_PAIRS = TILES // PAIR
+MX_ISSUES = 2
 
 FLOPS = 2 * ROWS * D_IN * GATES * D_HID + 2 * ROWS * D_HEAD * GATES * D_HID
 
@@ -205,11 +206,12 @@ def tile_slstmblock_pa_t_kernel(
                 for blk in range(BLOCKS):
                     cols = slice(blk * P, (blk + 1) * P)
                     mx_ps = psum_rot.tile([P, CHUNK], F32, tag="mx_ps")
-                    nc.tensor.matmul_mx(out=mx_ps[:],
-                                        lhsT=w_codes[:, cols].bitcast(FP8X4),
-                                        lhsT_scale=w_scales[:, cols],
-                                        rhs=x_codes[:].bitcast(FP8X4), rhs_scale=x_scales[:],
-                                        start=True, stop=True)
+                    for issue in range(MX_ISSUES):
+                        nc.tensor.matmul_mx(out=mx_ps[:],
+                                            lhsT=w_codes[:, cols].bitcast(FP8X4),
+                                            lhsT_scale=w_scales[:, cols],
+                                            rhs=x_codes[:].bitcast(FP8X4), rhs_scale=x_scales[:],
+                                            start=True, stop=True)
                     nc.scalar.activation(out=mx_turned[:, blk, :], in_=mx_ps[:], func=ACT.Identity,
                                          bias=gate_bias[:, blk:blk + 1], scale=1.0)
                 mt_tiles[s] = mx_turned

@@ -28,7 +28,6 @@ CHUNK = TILES * P
 N_CHUNKS = ROWS // CHUNK
 PAIR = 2
 N_PAIRS = TILES // PAIR
-MX_ISSUES = 2
 
 FLOPS = 2 * ROWS * D_IN * GATES * D_HID + 2 * ROWS * D_HEAD * GATES * D_HID
 
@@ -206,12 +205,11 @@ def tile_slstmblock_pa_t_kernel(
                 for blk in range(BLOCKS):
                     cols = slice(blk * P, (blk + 1) * P)
                     mx_ps = psum_rot.tile([P, CHUNK], F32, tag="mx_ps")
-                    for issue in range(MX_ISSUES):
-                        nc.tensor.matmul_mx(out=mx_ps[:],
-                                            lhsT=w_codes[:, cols].bitcast(FP8X4),
-                                            lhsT_scale=w_scales[:, cols],
-                                            rhs=x_codes[:].bitcast(FP8X4), rhs_scale=x_scales[:],
-                                            start=True, stop=True)
+                    nc.tensor.matmul_mx(out=mx_ps[:],
+                                        lhsT=w_codes[:, cols].bitcast(FP8X4),
+                                        lhsT_scale=w_scales[:, cols],
+                                        rhs=x_codes[:].bitcast(FP8X4), rhs_scale=x_scales[:],
+                                        start=True, stop=True)
                     nc.scalar.activation(out=mx_turned[:, blk, :], in_=mx_ps[:], func=ACT.Identity,
                                          bias=gate_bias[:, blk:blk + 1], scale=1.0)
                 mt_tiles[s] = mx_turned
@@ -220,19 +218,21 @@ def tile_slstmblock_pa_t_kernel(
                 mx_turned = mt_tiles[s]
                 h_turned = ht_tiles[s]
                 tiles = slice(q * PAIR, (q + 1) * PAIR)
+                quarters = [(jj, h) for jj in range(PAIR) for h in range(HEADS)]
                 pre = []
                 for g in range(GATES):
                     pre_g = psum_pre.tile([P, PAIR, D_HID], F32, tag="pre%d" % g, name="pre_g")
-                    for jj in range(PAIR):
+                    for n, (jj, h) in enumerate(quarters):
                         j = q * PAIR + jj
-                        for h in range(HEADS):
-                            out = pre_g[:, jj, h * D_HEAD:(h + 1) * D_HEAD]
-                            nc.tensor.matmul(out=out,
-                                             lhsT=mx_turned[:, g * HEADS + h, j * P:(j + 1) * P],
-                                             rhs=ident_f32[:], start=True, stop=False,
-                                             is_transpose=True)
-                            nc.tensor.matmul(out=out, lhsT=h_turned[:, h, j, :],
-                                             rhs=r_sb[:, g, h, :], start=False, stop=True)
+                        nc.tensor.matmul(out=pre_g[:, jj, h * D_HEAD:(h + 1) * D_HEAD],
+                                         lhsT=mx_turned[:, g * HEADS + h, j * P:(j + 1) * P],
+                                         rhs=ident_f32[:], start=(n == 0), stop=False,
+                                         is_transpose=True)
+                    for n, (jj, h) in enumerate(quarters):
+                        j = q * PAIR + jj
+                        nc.tensor.matmul(out=pre_g[:, jj, h * D_HEAD:(h + 1) * D_HEAD],
+                                         lhsT=h_turned[:, h, j, :], rhs=r_sb[:, g, h, :],
+                                         start=False, stop=(n == len(quarters) - 1))
                     pre.append(pre_g)
                 shape = [P, PAIR, D_HID]
                 zt = work.tile(shape, F32, tag="zt")

from contextlib import ExitStack

import concourse.mybir as mybir
from concourse.masks import make_identity

F32 = mybir.dt.float32
BF16 = mybir.dt.bfloat16
U32 = mybir.dt.uint32
U8 = mybir.dt.uint8
FP8X4 = mybir.dt.float8_e4m3fn_x4
ALU = mybir.AluOpType
ACT = mybir.ActivationFunctionType

P = 128
PACK = 4
ROWS = 4096
D_IN = 512
D_HID = 256
HEADS = 2
D_HEAD = 128
GATES = 4
BLOCKS = GATES * HEADS
LN_EPS = 1e-5
DIV_EPS = 1e-13

TILES = 4
CHUNK = TILES * P
N_CHUNKS = ROWS // CHUNK
PAIR = 2
N_PAIRS = TILES // PAIR

FLOPS = 2 * ROWS * D_IN * GATES * D_HID + 2 * ROWS * D_HEAD * GATES * D_HID


def tile_slstmblock_pa_t_kernel(
    tc, x, h_prev, c_prev, n_prev, m_prev, ln_w, ln_b,
    Wz, b_z, Rz, rb_z, Wi, b_i, Ri, rb_i, Wf, b_f, Rf, rb_f, Wo, b_o, Ro, rb_o,
    out_0, out_1, out_2, out_3,
):
    nc = tc.nc
    weights = [Wz, Wi, Wf, Wo]
    recurrents = [Rz, Ri, Rf, Ro]
    biases = [b_z, b_i, b_f, b_o]
    rec_biases = [rb_z, rb_i, rb_f, rb_o]
    GZ, GI, GF, GO = 0, 1, 2, 3

    def chunk_rows(dram, s):
        return dram[s * CHUNK:(s + 1) * CHUNK, :].rearrange("(p j) w -> p j w", j=TILES)

    with ExitStack() as stack:
        const = stack.enter_context(tc.tile_pool(name="const", bufs=1))
        keep = stack.enter_context(tc.tile_pool(name="keep", bufs=1))
        loads = stack.enter_context(tc.tile_pool(name="loads", bufs=2))
        psum_pre = stack.enter_context(tc.psum_pool(name="psum_pre", bufs=1))
        psum_rot = stack.enter_context(tc.psum_pool(name="psum_rot", bufs=2))

        ident_f32 = const.tile([P, P], F32)
        make_identity(nc, ident_f32[:])
        ident_bf16 = const.tile([P, P], BF16)
        make_identity(nc, ident_bf16[:])
        neg_half = const.tile([P, TILES], F32)
        nc.vector.memset(neg_half[:], -0.5)
        div_eps = const.tile([P, 1], F32)
        nc.vector.memset(div_eps[:], DIV_EPS)

        vec_rows = const.tile([P, P], BF16)
        nc.vector.memset(vec_rows[:], 0.0)
        nc.scalar.dma_start(out=vec_rows[0:4, :], in_=ln_w.rearrange("(t p) -> t p", p=P))
        nc.scalar.dma_start(out=vec_rows[4:8, :], in_=ln_b.rearrange("(t p) -> t p", p=P))
        for g in range(GATES):
            nc.scalar.dma_start(out=vec_rows[8 + HEADS * g:8 + HEADS * (g + 1), :],
                                in_=biases[g].rearrange("(h f) -> h f", f=D_HEAD))
            nc.scalar.dma_start(out=vec_rows[16 + HEADS * g:16 + HEADS * (g + 1), :],
                                in_=rec_biases[g].rearrange("(h f) -> h f", f=D_HEAD))

        x_tiles = {}
        h_tiles = {}
        c_tiles = {}
        n_tiles = {}
        m_tiles = {}

        def load_x(s):
            x_sb = loads.tile([P, TILES, D_IN], BF16, tag="x_sb", bufs=3)
            nc.sync.dma_start(out=x_sb[:], in_=chunk_rows(x, s))
            x_tiles[s] = x_sb

        def load_state(s):
            h_sb = loads.tile([P, TILES, D_HID], BF16, tag="h_sb")
            nc.sync.dma_start(out=h_sb[:], in_=chunk_rows(h_prev, s))
            h_tiles[s] = h_sb
            m_sb = loads.tile([P, TILES, D_HID], BF16, tag="m_sb")
            nc.sync.dma_start(out=m_sb[:], in_=chunk_rows(m_prev, s))
            m_tiles[s] = m_sb
            c_sb = loads.tile([P, TILES, D_HID], BF16, tag="c_sb")
            nc.sync.dma_start(out=c_sb[:], in_=chunk_rows(c_prev, s))
            c_tiles[s] = c_sb
            n_sb = loads.tile([P, TILES, D_HID], BF16, tag="n_sb")
            nc.sync.dma_start(out=n_sb[:], in_=chunk_rows(n_prev, s))
            n_tiles[s] = n_sb

        load_x(0)

        w_codes = const.tile([P, GATES * D_HID], U32, align_bytes=64)
        w_scales = const.tile([P, GATES * D_HID], U8, align_bytes=64)
        r_sb = const.tile([P, GATES, HEADS, D_HEAD], BF16)
        with tc.tile_pool(name="setup", bufs=2) as setup:
            for g in range(GATES):
                w_raw = setup.tile([P, PACK, D_HID], BF16)
                nc.sync.dma_start(out=w_raw[:], in_=weights[g].rearrange("(t p) f -> p t f", p=P))
                w_grouped = setup.tile([P, D_HID, PACK], BF16, align_bytes=64)
                nc.scalar.copy(out=w_grouped[:], in_=w_raw[:].rearrange("p t f -> p f t"))
                cols = slice(g * D_HID, (g + 1) * D_HID)
                nc.vector.quantize_mx(
                    out=w_codes[:, cols].bitcast(FP8X4),
                    scales=w_scales[:, cols],
                    in_=w_grouped[:].rearrange("p f t -> p (f t)"),
                )
        load_x(1)
        load_state(0)
        for g in range(GATES):
            nc.sync.dma_start(out=r_sb[:, g, :, :], in_=recurrents[g].rearrange("h k f -> k h f"))
        load_x(2)

        vec_ps = psum_rot.tile([P, P], BF16, tag="turn")
        nc.tensor.transpose(vec_ps[:], vec_rows[:], ident_bf16[:])
        vec_cols = const.tile([P, 24], F32)
        nc.vector.tensor_copy(out=vec_cols[:], in_=vec_ps[:, 0:24])
        gain = vec_cols[:, 0:4]
        shift = vec_cols[:, 4:8]
        gate_bias = const.tile([P, BLOCKS], F32)
        nc.vector.tensor_add(out=gate_bias[:], in0=vec_cols[:, 8:16], in1=vec_cols[:, 16:24])

        nt_keep = [keep.tile([P, TILES, D_HID], F32, name="nt_keep%d" % s) for s in range(N_CHUNKS)]
        oc_keep = [keep.tile([P, TILES, D_HID], F32, name="oc_keep%d" % s) for s in range(N_CHUNKS)]
        sg_keep = [keep.tile([P, TILES, D_HID], BF16, name="sg_keep%d" % s) for s in range(N_CHUNKS)]

        with ExitStack() as main_stack:
            products = main_stack.enter_context(
                tc.tile_pool(name="products", bufs=2, reuse_waits="tile"))
            work = main_stack.enter_context(tc.tile_pool(name="work", bufs=2, reuse_waits="tile"))
            xh_tiles = {}
            x_mx = {}
            ht_tiles = {}
            mt_tiles = {}
            m_out = {}
            c_out = {}

            def normalise(s):
                x_sb = x_tiles.pop(s)
                stats = work.tile([P, TILES, 6], F32, tag="stats")
                mean_var = work.tile([P, TILES, 2], F32, tag="mean_var")
                for j in range(TILES):
                    nc.vector.bn_stats(out=stats[:, j, :], in_=x_sb[:, j, :])
                for j in range(TILES):
                    nc.vector.bn_aggr(out=mean_var[:, j, :], in_=stats[:, j, :])
                var_eps = work.tile([P, TILES], F32, tag="var_eps")
                nc.vector.tensor_scalar_add(out=var_eps[:], in0=mean_var[:, :, 1], scalar1=LN_EPS)
                neg_mean = work.tile([P, TILES], F32, tag="neg_mean")
                nc.vector.tensor_scalar_mul(out=neg_mean[:], in0=mean_var[:, :, 0], scalar1=-1.0)
                rstd = work.tile([P, TILES], F32, tag="rstd")
                nc.gpsimd.tensor_tensor(out=rstd[:], in0=var_eps[:], in1=neg_half[:], op=ALU.pow)
                xh = []
                for j in range(TILES):
                    xh_j = work.tile([P, D_IN], F32, tag="xh", bufs=2 * TILES)
                    nc.gpsimd.tensor_scalar(out=xh_j[:], in0=x_sb[:, j, :],
                                            scalar1=neg_mean[:, j:j + 1], scalar2=rstd[:, j:j + 1],
                                            op0=ALU.add, op1=ALU.mult)
                    xh.append(xh_j)
                xh_tiles[s] = xh

            def quantise_xn(s):
                xh = xh_tiles.pop(s)
                xn_planes = work.tile([P, PACK, CHUNK], BF16, tag="xn_planes", bufs=1)
                for t in range(PACK):
                    turned = psum_rot.tile([P, CHUNK], F32, tag="turn")
                    for j in range(TILES):
                        nc.tensor.transpose(turned[:, j * P:(j + 1) * P],
                                            xh[j][:, t * P:(t + 1) * P], ident_f32[:])
                    nc.scalar.activation(out=xn_planes[:, t, :], in_=turned[:], func=ACT.Identity,
                                         bias=shift[:, t:t + 1], scale=gain[:, t:t + 1])
                xn_grouped = work.tile([P, CHUNK, PACK], BF16, tag="xn_grouped", bufs=1,
                                       align_bytes=64)
                nc.vector.tensor_copy(out=xn_grouped[:].rearrange("p (c i) t -> p c t i", i=4),
                                      in_=xn_planes[:].rearrange("p t (c i) -> p c t i", i=4))
                x_codes = work.tile([P, CHUNK], U32, tag="x_codes", bufs=3, align_bytes=64)
                x_scales = work.tile([P, CHUNK], U8, tag="x_scales", bufs=3, align_bytes=64)
                nc.vector.quantize_mx(out=x_codes[:].bitcast(FP8X4), scales=x_scales[:],
                                      in_=xn_grouped[:].rearrange("p r t -> p (r t)"))
                x_mx[s] = (x_codes, x_scales)

            def turn_h(s):
                h_sb = h_tiles.pop(s)
                h_ps = psum_rot.tile([P, HEADS, TILES, P], BF16, tag="turn")
                for h in range(HEADS):
                    for j in range(TILES):
                        nc.tensor.transpose(h_ps[:, h, j, :],
                                            h_sb[:, j, h * D_HEAD:(h + 1) * D_HEAD], ident_bf16[:])
                h_turned = work.tile([P, HEADS, TILES, P], BF16, tag="h_turned")
                nc.scalar.copy(out=h_turned[:], in_=h_ps[:])
                ht_tiles[s] = h_turned

            def gate_products(s):
                x_codes, x_scales = x_mx.pop(s)
                mx_turned = products.tile([P, BLOCKS, CHUNK], F32, tag="mx_turned")
                for blk in range(BLOCKS):
                    cols = slice(blk * P, (blk + 1) * P)
                    mx_ps = psum_rot.tile([P, CHUNK], F32, tag="mx_ps")
                    nc.tensor.matmul_mx(out=mx_ps[:],
                                        lhsT=w_codes[:, cols].bitcast(FP8X4),
                                        lhsT_scale=w_scales[:, cols],
                                        rhs=x_codes[:].bitcast(FP8X4), rhs_scale=x_scales[:],
                                        start=True, stop=True)
                    nc.scalar.activation(out=mx_turned[:, blk, :], in_=mx_ps[:], func=ACT.Identity,
                                         bias=gate_bias[:, blk:blk + 1], scale=1.0)
                mt_tiles[s] = mx_turned

            def gating(s, q):
                mx_turned = mt_tiles[s]
                h_turned = ht_tiles[s]
                tiles = slice(q * PAIR, (q + 1) * PAIR)
                quarters = [(jj, h) for jj in range(PAIR) for h in range(HEADS)]
                pre = []
                for g in range(GATES):
                    pre_g = psum_pre.tile([P, PAIR, D_HID], F32, tag="pre%d" % g, name="pre_g")
                    for n, (jj, h) in enumerate(quarters):
                        j = q * PAIR + jj
                        nc.tensor.matmul(out=pre_g[:, jj, h * D_HEAD:(h + 1) * D_HEAD],
                                         lhsT=mx_turned[:, g * HEADS + h, j * P:(j + 1) * P],
                                         rhs=ident_f32[:], start=(n == 0), stop=False,
                                         is_transpose=True)
                    for n, (jj, h) in enumerate(quarters):
                        j = q * PAIR + jj
                        nc.tensor.matmul(out=pre_g[:, jj, h * D_HEAD:(h + 1) * D_HEAD],
                                         lhsT=h_turned[:, h, j, :], rhs=r_sb[:, g, h, :],
                                         start=False, stop=(n == len(quarters) - 1))
                    pre.append(pre_g)
                shape = [P, PAIR, D_HID]
                zt = work.tile(shape, F32, tag="zt")
                nc.scalar.activation(out=zt[:], in_=pre[GZ][:], func=ACT.Tanh)
                th = work.tile(shape, F32, tag="th")
                nc.scalar.activation(out=th[:], in_=pre[GO][:], func=ACT.Tanh, scale=0.5)
                fm = work.tile(shape, F32, tag="fm")
                nc.vector.tensor_tensor(out=fm[:], in0=pre[GF][:], in1=m_tiles[s][:, tiles, :],
                                        op=ALU.add)
                diff = work.tile(shape, F32, tag="diff")
                nc.vector.tensor_tensor(out=diff[:], in0=pre[GI][:], in1=fm[:], op=ALU.subtract)
                if q == 0:
                    m_out[s] = work.tile([P, TILES, D_HID], F32, tag="m_stage", name="m_stage")
                    c_out[s] = work.tile([P, TILES, D_HID], F32, tag="c_stage", name="c_stage")
                nc.vector.tensor_tensor(out=m_out[s][:, tiles, :], in0=pre[GI][:], in1=fm[:],
                                        op=ALU.max)
                e_i = work.tile(shape, F32, tag="e_i")
                nc.scalar.activation(out=e_i[:], in_=diff[:], func=ACT.Exp)
                e_f = work.tile(shape, F32, tag="e_f")
                nc.scalar.activation(out=e_f[:], in_=diff[:], func=ACT.Exp, scale=-1.0)
                ct = c_out[s][:, tiles, :]
                nt = nt_keep[s][:, tiles, :]
                iz = work.tile(shape, F32, tag="iz", bufs=1)
                nc.vector.scalar_tensor_tensor(out=ct, in0=e_f[:], scalar=1.0,
                                               in1=c_tiles[s][:, tiles, :],
                                               op0=ALU.min, op1=ALU.mult)
                nc.vector.scalar_tensor_tensor(out=nt, in0=e_f[:], scalar=1.0,
                                               in1=n_tiles[s][:, tiles, :],
                                               op0=ALU.min, op1=ALU.mult)
                nc.vector.scalar_tensor_tensor(out=iz[:], in0=e_i[:], scalar=1.0, in1=zt[:],
                                               op0=ALU.min, op1=ALU.mult)
                nc.vector.scalar_tensor_tensor(out=nt, in0=e_i[:], scalar=1.0, in1=nt,
                                               op0=ALU.min, op1=ALU.add)
                nc.vector.tensor_tensor(out=ct, in0=ct, in1=iz[:], op=ALU.add)
                nc.scalar.activation(out=sg_keep[s][:, tiles, :], in_=nt, func=ACT.Sign,
                                     bias=div_eps[:, 0:1], scale=1.0)
                nc.vector.scalar_tensor_tensor(out=oc_keep[s][:, tiles, :], in0=th[:], scalar=1.0,
                                               in1=ct, op0=ALU.add, op1=ALU.mult)

            def store_chunk(s):
                nc.sync.dma_start(out=chunk_rows(out_3, s), in_=m_out.pop(s)[:])
                nc.sync.dma_start(out=chunk_rows(out_2, s), in_=nt_keep[s][:])
                nc.sync.dma_start(out=chunk_rows(out_1, s), in_=c_out.pop(s)[:])

            normalise(0)
            normalise(1)
            quantise_xn(0)
            turn_h(0)
            gate_products(0)
            for s in range(N_CHUNKS):
                if s + 3 < N_CHUNKS:
                    load_x(s + 3)
                if s + 1 < N_CHUNKS:
                    load_state(s + 1)
                if s + 2 < N_CHUNKS:
                    normalise(s + 2)
                if s + 1 < N_CHUNKS:
                    quantise_xn(s + 1)
                    turn_h(s + 1)
                    gate_products(s + 1)
                gating(s, 0)
                gating(s, 1)
                store_chunk(s)

        with tc.tile_pool(name="tail", bufs=3, reuse_waits="tile") as tail:
            halves = [slice(q * PAIR, (q + 1) * PAIR) for q in range(N_PAIRS)]
            for s in range(N_CHUNKS):
                inv = tail.tile([P, TILES, D_HID], F32)
                h_stage = tail.tile([P, TILES, D_HID], F32)
                for tiles in halves:
                    nc.scalar.activation(out=inv[:, tiles, :], in_=nt_keep[s][:, tiles, :],
                                         func=ACT.Abs_reciprocal_sqrt, bias=div_eps[:, 0:1], scale=1.0)
                for tiles in halves:
                    nc.scalar.activation(out=inv[:, tiles, :], in_=inv[:, tiles, :], func=ACT.Square)
                for tiles in halves:
                    nc.vector.scalar_tensor_tensor(out=inv[:, tiles, :], in0=oc_keep[s][:, tiles, :],
                                                   scalar=0.5, in1=inv[:, tiles, :],
                                                   op0=ALU.mult, op1=ALU.mult)
                for tiles in halves:
                    nc.vector.tensor_tensor(out=h_stage[:, tiles, :], in0=inv[:, tiles, :],
                                            in1=sg_keep[s][:, tiles, :], op=ALU.mult)
                nc.sync.dma_start(out=chunk_rows(out_0, s), in_=h_stage[:])
